import numpy as np
import ml_dtypes


def mxq(x, axis, fmt="e4m3"):
    dtype, down = {"e4m3": (ml_dtypes.float8_e4m3fn, 7), "e5m2": (ml_dtypes.float8_e5m2, 14)}[fmt]
    v = np.moveaxis(np.asarray(x, np.float32).astype(ml_dtypes.bfloat16).astype(np.float64), axis, -1)
    blocks = v.reshape(v.shape[:-1] + (-1, 32))
    amax = np.abs(blocks).max(-1, keepdims=True)
    byte = np.maximum(np.where(amax > 0, np.frexp(amax)[1] - 1 + 127, 0) - down, 1)
    scale = np.exp2(byte - 127.0)
    codes = (blocks / scale).astype(np.float32).astype(dtype).astype(np.float64)
    return np.moveaxis((codes * scale).reshape(v.shape), -1, axis)


WIDE = False


def mx_kscale(k):
    if not WIDE:
        return np.ones(k)
    levels = np.array([10, -10, 5, -5, 0])
    a = np.random.permutation(np.resize(levels, k // 512 * 4)).reshape(k // 512, 4)
    idx = np.arange(k)
    return np.exp2(a[idx // 512, idx % 128 // 32])


BF16 = ml_dtypes.bfloat16


def bf(x):
    return np.asarray(x, np.float32).astype(BF16)


def f64(x):
    return np.asarray(x).astype(np.float64)


B, T, HIDDEN, NUM_HEADS, HEAD_DIM, ROT_DIM, LATENT = 2, 512, 2048, 16, 128, 64, 512
NOPE_DIM = HEAD_DIM - ROT_DIM
BASE = 10000.0


def rope_tables():
    inv_freq = 1.0 / (BASE ** (np.arange(0, ROT_DIM, 2) / ROT_DIM))
    freqs = np.arange(T)[:, None] * inv_freq[None, :]
    emb = np.concatenate((freqs, freqs), axis=-1)
    return np.cos(emb), np.sin(emb)


def rotate_half(v):
    v1, v2 = v[..., : v.shape[-1] // 2], v[..., v.shape[-1] // 2 :]
    return np.concatenate((-v2, v1), axis=-1)


def heads(y, d):
    return y.reshape(B, T, NUM_HEADS, d).transpose(0, 2, 1, 3)


def setup_inputs():
    s, t = mx_kscale(HIDDEN), mx_kscale(LATENT)
    cos, sin = rope_tables()
    return {"x": bf(np.random.standard_normal((B, T, HIDDEN)) * s),
            "Wq_d": bf(np.random.standard_normal((HIDDEN, LATENT)) / np.sqrt(HIDDEN) / s[:, None] * t),
            "Wq_nope": bf(np.random.standard_normal((LATENT, NUM_HEADS * NOPE_DIM)) / np.sqrt(LATENT) / t[:, None]),
            "Wrq": bf(np.random.standard_normal((LATENT, NUM_HEADS * ROT_DIM)) / np.sqrt(LATENT) / t[:, None]),
            "cos": bf(cos), "sin": bf(sin)}


def reference(x, Wq_d, Wq_nope, Wrq, cos, sin):
    q_latent = mxq(f64(x), 2, "e4m3") @ mxq(f64(Wq_d), 0, "e4m3")
    lq = mxq(q_latent, 2, "e4m3")
    q_nope = heads(lq @ mxq(f64(Wq_nope), 0, "e4m3"), NOPE_DIM)
    q_rot = heads(lq @ mxq(f64(Wrq), 0, "e4m3"), ROT_DIM)
    c, sn = f64(cos)[None, None, :, :], f64(sin)[None, None, :, :]
    q_rot = q_rot * c + rotate_half(q_rot) * sn
    return np.concatenate([q_rot, q_nope], axis=-1)

@@ -1,0 +1,378 @@
+from contextlib import ExitStack
+
+import concourse.mybir as mybir
+from concourse.masks import make_identity
+
+F32 = mybir.dt.float32
+BF16 = mybir.dt.bfloat16
+U32 = mybir.dt.uint32
+U8 = mybir.dt.uint8
+FP8X4 = mybir.dt.float8_e4m3fn_x4
+MULT = mybir.AluOpType.mult
+ADD = mybir.AluOpType.add
+
+P = 128
+FLOPS = 2 * 1024 * 2048 * 512 + 2 * 1024 * 512 * 2048
+
+SCALAR_COLS = {"wd0": 256, "wd1": 256, "wd2": 256, "wd3": 256, "rq0": 176, "rq1": 176, "np0": 336, "np1": 336}
+
+def tile_multiheadlatentattention_pa_kernel(tc, x, Wq_d, Wq_nope, Wrq, cos, sin, out):
+    nc = tc.nc
+    with ExitStack() as ctx:
+        const = ctx.enter_context(tc.tile_pool(name="const", bufs=1))
+        raw = ctx.enter_context(tc.tile_pool(name="raw", bufs=1))
+        grp = ctx.enter_context(tc.tile_pool(name="grp", bufs=3))
+        mx = ctx.enter_context(tc.tile_pool(name="mx", bufs=1))
+        prod = ctx.enter_context(tc.tile_pool(name="prod", bufs=3))
+        res = ctx.enter_context(tc.tile_pool(name="res", bufs=4))
+        ps_x = ctx.enter_context(tc.psum_pool(name="ps_x", bufs=2))
+        ps_q = ctx.enter_context(tc.psum_pool(name="ps_q", bufs=1))
+        ps_r = ctx.enter_context(tc.psum_pool(name="ps_r", bufs=3))
+        ps_n = ctx.enter_context(tc.psum_pool(name="ps_n", bufs=2))
+        ctx.enter_context(tc.manual_schedule())
+
+        ident = const.tile([P, P], F32, name="ident")
+        make_identity(nc, ident[:])
+        cs = const.tile([P, 2, 256], BF16, name="cs")
+        nc.scalar.dma_start(out=cs[:, 0, :], in_=cos.rearrange("(p i) d -> p (i d)", i=4))
+        nc.scalar.dma_start(out=cs[:, 1, :], in_=sin.rearrange("(p i) d -> p (i d)", i=4))
+        ct = const.tile([P, 4, 2, 64], F32, name="ct")
+
+        tiles = {}
+        w_src = {"rq": Wrq, "np": Wq_nope}
+
+        def load(name):
+            if name[0] == "x":
+                n = int(name[1])
+                b, i = divmod(n, 4)
+                t = raw.tile([P, 2048], BF16, name="raw_" + name)
+                nc.sync.dma_start(out=t[:], in_=x[b].rearrange("(p i) k -> p i k", i=4)[:, i, :])
+            elif name[0] == "w":
+                g = int(name[2])
+                t = raw.tile([P, 4, 512], BF16, name="raw_" + name)
+                nc.sync.dma_start(
+                    out=t[:].rearrange("q (u e) c -> q u (e c)", u=2),
+                    in_=Wq_d[512 * g : 512 * (g + 1), :].rearrange("(u q e) c -> q u (e c)", u=2, e=2),
+                )
+            else:
+                t = raw.tile([P, 4, 1024], BF16, name="raw_" + name)
+                nc.sync.dma_start(out=t[:], in_=w_src[name].rearrange("(t p) n -> p t n", p=P))
+            tiles["raw_" + name] = t
+
+        def tables():
+            cv = cs[:, 0, :].rearrange("p (i d) -> p i d", d=64)
+            sv = cs[:, 1, :].rearrange("p (i d) -> p i d", d=64)
+            nc.vector.tensor_copy(out=ct[:, :, 0, :], in_=cv)
+            nc.vector.tensor_copy(out=ct[:, :, 1, 0:32], in_=sv[:, :, 32:64])
+            nc.vector.tensor_scalar_mul(out=ct[:, :, 1, 32:64], in0=sv[:, :, 0:32], scalar1=-1.0)
+
+        def get(key, pool, shape, dtype, tag):
+            if key not in tiles:
+                tiles[key] = pool.tile(shape, dtype, tag=tag, name=key, align_bytes=64)
+            return tiles[key]
+
+        def getp(key, pool, shape, tag):
+            if key not in tiles:
+                tiles[key] = pool.tile(shape, F32, tag=tag, name=key)
+            return tiles[key]
+
+        def regroup(eng, name):
+            if name[0] == "w":
+                src = tiles["raw_" + name][:]
+            else:
+                hg = int(name[2])
+                src = tiles["raw_" + name[0:2]][:, :, 512 * hg : 512 * (hg + 1)]
+            v = 512 - SCALAR_COLS[name]
+            d = get("g_" + name, grp, [P, 2048], BF16, "gw")[:].rearrange("p (c t) -> p c t", t=4)
+            if eng == "V":
+                nc.vector.tensor_copy(
+                    out=d[:, 0:v, :].rearrange("p (c i) t -> p c t i", i=4),
+                    in_=src[:, :, 0:v].rearrange("p t (c i) -> p c t i", i=4),
+                )
+            else:
+                nc.scalar.copy(
+                    out=d[:, v:512, :].rearrange("p (c i) t -> p c t i", i=4),
+                    in_=src[:, :, v:512].rearrange("p t (c i) -> p c t i", i=4),
+                )
+
+        def quantise(name, words):
+            codes = mx.tile([P, words], U32, name="c_" + name, align_bytes=64)
+            scales = mx.tile([P, words], U8, name="s_" + name, align_bytes=64)
+            nc.vector.quantize_mx(out=codes[:].bitcast(FP8X4), scales=scales[:], in_=tiles["g_" + name][:])
+            tiles["c_" + name] = codes
+            tiles["s_" + name] = scales
+
+        def x_t(n, hb):
+            xw = tiles["raw_x%d" % n][:].bitcast(F32)
+            xt = getp("xt%d_%d" % (n, hb), ps_x, [P, 4, P], "xt")
+            for w in range(4):
+                c0 = P * (4 * hb + w)
+                nc.tensor.transpose(xt[:, w, :], xw[:, c0 : c0 + P], ident[:])
+
+        def x_c(n, hb):
+            gx = get("g_x%d" % n, grp, [P, 2048], BF16, "gx")
+            gxw = gx[:].bitcast(F32).rearrange("q (g p u) -> q g p u", g=4, u=2)
+            nc.scalar.copy(
+                out=gxw[:, 2 * hb : 2 * hb + 2],
+                in_=tiles["xt%d_%d" % (n, hb)][:].rearrange("q (g u) p -> q g p u", u=2),
+            )
+
+        def s1(n):
+            qp = getp("qp%d" % n, ps_q, [P, 4, P], "qp")
+            for j in range(4):
+                for g in range(4):
+                    nc.tensor.matmul_mx(
+                        out=qp[:, j, :],
+                        lhsT=tiles["c_wd%d" % g][:, P * j : P * (j + 1)].bitcast(FP8X4),
+                        lhsT_scale=tiles["s_wd%d" % g][:, P * j : P * (j + 1)],
+                        rhs=tiles["c_x%d" % n][:, P * g : P * (g + 1)].bitcast(FP8X4),
+                        rhs_scale=tiles["s_x%d" % n][:, P * g : P * (g + 1)],
+                        start=(g == 0),
+                        stop=(g == 3),
+                    )
+
+        def q_c(n):
+            gq = get("g_q%d" % n, grp, [P, 512], BF16, "gq")
+            nc.scalar.copy(
+                out=gq[:].rearrange("p (n j) -> p n j", j=4),
+                in_=tiles["qp%d" % n][:].rearrange("p j n -> p n j"),
+            )
+
+        def s2(kind, pool, n, hg):
+            acc = getp("%s%d_%d" % (kind, n, hg), pool, [P, 512], kind)
+            nc.tensor.matmul_mx(
+                out=acc[:],
+                lhsT=tiles["c_q%d" % n][:].bitcast(FP8X4),
+                lhsT_scale=tiles["s_q%d" % n][:],
+                rhs=tiles["c_%s%d" % (kind, hg)][:].bitcast(FP8X4),
+                rhs_scale=tiles["s_%s%d" % (kind, hg)][:],
+                start=True,
+                stop=True,
+            )
+
+        def r_v(n, hg):
+            a = get("ab%d_%d" % (n // 2, hg), prod, [P, 2, 2, 512], F32, "ab")
+            nc.vector.tensor_tensor(
+                out=a[:, n % 2].rearrange("p a (h d) -> p a h d", d=64),
+                in0=tiles["rq%d_%d" % (n, hg)][:].rearrange("p (h d) -> p h d", d=64).unsqueeze(1).to_broadcast([P, 2, 8, 64]),
+                in1=ct[:, n % 4].unsqueeze(2).to_broadcast([P, 2, 8, 64]),
+                op=MULT,
+            )
+
+        def n_c(n, hg):
+            o = get("ot%d_%d" % (n // 2, hg), res, [P, 8, 2, P], F32, "ot")
+            nc.scalar.copy(
+                out=o[:, :, n % 2, 64:128],
+                in_=tiles["np%d_%d" % (n, hg)][:].rearrange("p (h d) -> p h d", d=64),
+            )
+
+        def add(eng, s, hg, half):
+            o = get("ot%d_%d" % (s, hg), res, [P, 8, 2, P], F32, "ot")
+            a = tiles["ab%d_%d" % (s, hg)]
+            lo = 32 * half
+            sw = 32 * (1 - half)
+            eng.tensor_tensor(
+                out=o[:, :, :, lo : lo + 32].rearrange("p h s d -> p s h d"),
+                in0=a[:, :, 0].rearrange("p s (h d) -> p s h d", d=64)[:, :, :, lo : lo + 32],
+                in1=a[:, :, 1].rearrange("p s (h d) -> p s h d", d=64)[:, :, :, sw : sw + 32],
+                op=ADD,
+            )
+
+        def store(s, hg):
+            b, ip = divmod(s, 2)
+            nc.sync.dma_start(
+                out=out[b, 8 * hg : 8 * hg + 8].rearrange("h (p i) d -> p h (i d)", i=4)[:, :, 256 * ip : 256 * (ip + 1)],
+                in_=tiles["ot%d_%d" % (s, hg)][:].rearrange("p h s d -> p h (s d)"),
+            )
+
+        load("x0")
+        load("wd0")
+        load("wd1")
+        load("wd2")
+        load("wd3")
+        load("rq")
+        load("x1")
+        load("x2")
+        load("np")
+        load("x3")
+        load("x4")
+        load("x5")
+        load("x6")
+        load("x7")
+        tables()
+        x_t(0, 1)
+        x_t(0, 0)
+        x_c(0, 1)
+        x_c(0, 0)
+        regroup("V", "wd0")
+        regroup("S", "wd0")
+        quantise("x0", 512)
+        regroup("V", "wd1")
+        regroup("S", "wd1")
+        quantise("wd0", 512)
+        regroup("V", "wd2")
+        regroup("S", "wd2")
+        quantise("wd1", 512)
+        regroup("V", "wd3")
+        regroup("S", "wd3")
+        quantise("wd2", 512)
+        quantise("wd3", 512)
+        s1(0)
+        regroup("V", "rq0")
+        regroup("S", "rq0")
+        regroup("V", "rq1")
+        regroup("S", "rq1")
+        x_t(1, 1)
+        x_t(1, 0)
+        quantise("rq0", 512)
+        q_c(0)
+        quantise("rq1", 512)
+        x_c(1, 0)
+        x_t(2, 0)
+        x_c(1, 1)
+        quantise("q0", P)
+        s2("rq", ps_r, 0, 0)
+        x_c(2, 0)
+        quantise("x1", 512)
+        x_t(2, 1)
+        s2("rq", ps_r, 0, 1)
+        x_c(2, 1)
+        r_v(0, 0)
+        s1(1)
+        regroup("S", "np0")
+        regroup("V", "np0")
+        quantise("x2", 512)
+        x_t(3, 1)
+        q_c(1)
+        x_t(3, 0)
+        r_v(0, 1)
+        s1(2)
+        x_c(3, 0)
+        x_c(3, 1)
+        quantise("q1", P)
+        quantise("np0", 512)
+        regroup("S", "np1")
+        x_t(4, 0)
+        quantise("x3", 512)
+        s2("rq", ps_r, 1, 1)
+        x_t(4, 1)
+        regroup("V", "np1")
+        s2("np", ps_n, 1, 0)
+        r_v(1, 1)
+        s2("rq", ps_r, 1, 0)
+        n_c(1, 0)
+        s2("np", ps_n, 0, 0)
+        n_c(0, 0)
+        r_v(1, 0)
+        add(nc.gpsimd, 0, 1, 0)
+        q_c(2)
+        s1(3)
+        x_c(4, 1)
+        quantise("q2", P)
+        quantise("np1", 512)
+        x_c(4, 0)
+        add(nc.gpsimd, 0, 0, 1)
+        s2("rq", ps_r, 2, 0)
+        quantise("x4", 512)
+        q_c(3)
+        s2("np", ps_n, 0, 1)
+        s2("np", ps_n, 1, 1)
+        r_v(2, 0)
+        n_c(0, 1)
+        add(nc.gpsimd, 0, 0, 0)
+        x_t(5, 0)
+        s1(4)
+        n_c(1, 1)
+        quantise("q3", P)
+        x_c(5, 0)
+        add(nc.gpsimd, 0, 1, 1)
+        store(0, 0)
+        s2("rq", ps_r, 3, 0)
+        q_c(4)
+        x_t(5, 1)
+        r_v(3, 0)
+        s2("np", ps_n, 3, 0)
+        x_c(5, 1)
+        s2("rq", ps_r, 2, 1)
+        x_t(6, 1)
+        n_c(3, 0)
+        quantise("x5", 512)
+        x_t(6, 0)
+        add(nc.gpsimd, 1, 0, 0)
+        x_c(6, 1)
+        s2("np", ps_n, 2, 0)
+        r_v(2, 1)
+        s2("np", ps_n, 2, 1)
+        store(0, 1)
+        s2("rq", ps_r, 3, 1)
+        n_c(2, 0)
+        s1(5)
+        add(nc.gpsimd, 1, 0, 1)
+        n_c(2, 1)
+        r_v(3, 1)
+        x_c(6, 0)
+        x_t(7, 0)
+        q_c(5)
+        s2("np", ps_n, 3, 1)
+        quantise("q4", P)
+        add(nc.gpsimd, 1, 1, 1)
+        quantise("x6", 512)
+        x_t(7, 1)
+        n_c(3, 1)
+        s2("rq", ps_r, 4, 0)
+        store(1, 0)
+        quantise("q5", P)
+        s2("np", ps_n, 4, 1)
+        r_v(4, 0)
+        x_c(7, 0)
+        s2("np", ps_n, 4, 0)
+        s2("rq", ps_r, 5, 0)
+        add(nc.gpsimd, 1, 1, 0)
+        x_c(7, 1)
+        s1(6)
+        r_v(5, 0)
+        n_c(4, 1)
+        n_c(4, 0)
+        s2("np", ps_n, 5, 0)
+        s2("rq", ps_r, 5, 1)
+        quantise("x7", 512)
+        q_c(6)
+        add(nc.gpsimd, 2, 0, 0)
+        store(1, 1)
+        s2("np", ps_n, 5, 1)
+        s2("rq", ps_r, 4, 1)
+        n_c(5, 0)
+        r_v(5, 1)
+        s1(7)
+        n_c(5, 1)
+        add(nc.gpsimd, 2, 0, 1)
+        quantise("q6", P)
+        r_v(4, 1)
+        s2("rq", ps_r, 6, 0)
+        q_c(7)
+        s2("np", ps_n, 6, 0)
+        s2("rq", ps_r, 6, 1)
+        store(2, 0)
+        n_c(6, 0)
+        quantise("q7", P)
+        s2("np", ps_n, 6, 1)
+        add(nc.gpsimd, 2, 1, 1)
+        r_v(6, 0)
+        n_c(6, 1)
+        s2("np", ps_n, 7, 0)
+        s2("rq", ps_r, 7, 0)
+        n_c(7, 0)
+        s2("np", ps_n, 7, 1)
+        r_v(7, 0)
+        s2("rq", ps_r, 7, 1)
+        add(nc.gpsimd, 2, 1, 0)
+        n_c(7, 1)
+        r_v(6, 1)
+        add(nc.gpsimd, 3, 0, 0)
+        store(2, 1)
+        r_v(7, 1)
+        add(nc.gpsimd, 3, 0, 1)
+        add(nc.vector, 3, 1, 0)
+        add(nc.vector, 3, 1, 1)
+        store(3, 0)
+        store(3, 1)

@@ -14,7 +14,7 @@ ADD = mybir.AluOpType.add
 P = 128
 FLOPS = 2 * 1024 * 2048 * 512 + 2 * 1024 * 512 * 2048
 
-SCALAR_COLS = {"wd0": 256, "wd1": 256, "wd2": 256, "wd3": 256, "rq0": 176, "rq1": 176, "np0": 336, "np1": 336}
+SCALAR_COLS = {"wd0": 176, "wd1": 176, "wd2": 176, "wd3": 176, "rq0": 176, "rq1": 176, "np0": 176, "np1": 176}
 
 def tile_multiheadlatentattention_pa_kernel(tc, x, Wq_d, Wq_nope, Wrq, cos, sin, out):
     nc = tc.nc
@@ -29,7 +29,7 @@ def tile_multiheadlatentattention_pa_kernel(tc, x, Wq_d, Wq_nope, Wrq, cos, sin,
         ps_q = ctx.enter_context(tc.psum_pool(name="ps_q", bufs=1))
         ps_r = ctx.enter_context(tc.psum_pool(name="ps_r", bufs=3))
         ps_n = ctx.enter_context(tc.psum_pool(name="ps_n", bufs=2))
-        ctx.enter_context(tc.manual_schedule())
+
 
         ident = const.tile([P, P], F32, name="ident")
         make_identity(nc, ident[:])
@@ -190,20 +190,20 @@ def tile_multiheadlatentattention_pa_kernel(tc, x, Wq_d, Wq_nope, Wrq, cos, sin,
         load("wd1")
         load("wd2")
         load("wd3")
-        load("rq")
         load("x1")
-        load("x2")
+        load("rq")
         load("np")
+        load("x2")
         load("x3")
         load("x4")
         load("x5")
         load("x6")
         load("x7")
         tables()
-        x_t(0, 1)
         x_t(0, 0)
-        x_c(0, 1)
+        x_t(0, 1)
         x_c(0, 0)
+        x_c(0, 1)
         regroup("V", "wd0")
         regroup("S", "wd0")
         quantise("x0", 512)
@@ -216,163 +216,163 @@ def tile_multiheadlatentattention_pa_kernel(tc, x, Wq_d, Wq_nope, Wrq, cos, sin,
         regroup("V", "wd3")
         regroup("S", "wd3")
         quantise("wd2", 512)
+        x_t(1, 0)
+        x_t(1, 1)
+        x_c(1, 0)
+        x_c(1, 1)
         quantise("wd3", 512)
         s1(0)
+        quantise("x1", 512)
         regroup("V", "rq0")
         regroup("S", "rq0")
+        quantise("rq0", 512)
         regroup("V", "rq1")
         regroup("S", "rq1")
-        x_t(1, 1)
-        x_t(1, 0)
-        quantise("rq0", 512)
         q_c(0)
-        quantise("rq1", 512)
-        x_c(1, 0)
-        x_t(2, 0)
-        x_c(1, 1)
-        quantise("q0", P)
-        s2("rq", ps_r, 0, 0)
-        x_c(2, 0)
-        quantise("x1", 512)
-        x_t(2, 1)
-        s2("rq", ps_r, 0, 1)
-        x_c(2, 1)
-        r_v(0, 0)
         s1(1)
-        regroup("S", "np0")
-        regroup("V", "np0")
-        quantise("x2", 512)
-        x_t(3, 1)
+        quantise("q0", P)
+        quantise("rq1", 512)
+        s2("rq", ps_r, 0, 0)
+        s2("rq", ps_r, 0, 1)
+        x_t(2, 0)
+        x_t(2, 1)
+        r_v(0, 0)
         q_c(1)
+        x_c(2, 0)
+        x_c(2, 1)
         x_t(3, 0)
-        r_v(0, 1)
+        x_t(3, 1)
+        regroup("V", "np0")
+        regroup("S", "np0")
+        quantise("q1", P)
+        s2("rq", ps_r, 1, 0)
+        s2("rq", ps_r, 1, 1)
+        quantise("x2", 512)
         s1(2)
+        r_v(0, 1)
+        quantise("np0", 512)
+        regroup("V", "np1")
+        regroup("S", "np1")
         x_c(3, 0)
         x_c(3, 1)
-        quantise("q1", P)
-        quantise("np0", 512)
-        regroup("S", "np1")
-        x_t(4, 0)
-        quantise("x3", 512)
-        s2("rq", ps_r, 1, 1)
-        x_t(4, 1)
-        regroup("V", "np1")
-        s2("np", ps_n, 1, 0)
-        r_v(1, 1)
-        s2("rq", ps_r, 1, 0)
-        n_c(1, 0)
-        s2("np", ps_n, 0, 0)
-        n_c(0, 0)
-        r_v(1, 0)
-        add(nc.gpsimd, 0, 1, 0)
         q_c(2)
+        quantise("x3", 512)
+        quantise("np1", 512)
+        x_t(4, 0)
+        x_t(4, 1)
+        s2("np", ps_n, 0, 0)
+        s2("np", ps_n, 0, 1)
         s1(3)
+        r_v(1, 0)
+        n_c(0, 0)
+        x_c(4, 0)
         x_c(4, 1)
         quantise("q2", P)
-        quantise("np1", 512)
-        x_c(4, 0)
-        add(nc.gpsimd, 0, 0, 1)
         s2("rq", ps_r, 2, 0)
-        quantise("x4", 512)
-        q_c(3)
-        s2("np", ps_n, 0, 1)
-        s2("np", ps_n, 1, 1)
-        r_v(2, 0)
-        n_c(0, 1)
-        add(nc.gpsimd, 0, 0, 0)
-        x_t(5, 0)
-        s1(4)
-        n_c(1, 1)
-        quantise("q3", P)
-        x_c(5, 0)
-        add(nc.gpsimd, 0, 1, 1)
-        store(0, 0)
-        s2("rq", ps_r, 3, 0)
-        q_c(4)
-        x_t(5, 1)
-        r_v(3, 0)
-        s2("np", ps_n, 3, 0)
-        x_c(5, 1)
         s2("rq", ps_r, 2, 1)
-        x_t(6, 1)
-        n_c(3, 0)
+        r_v(1, 1)
+        n_c(0, 1)
+        q_c(3)
+        quantise("x4", 512)
+        x_t(5, 0)
+        x_t(5, 1)
+        s2("np", ps_n, 1, 0)
+        s2("np", ps_n, 1, 1)
+        add(nc.gpsimd, 0, 0, 0)
+        add(nc.gpsimd, 0, 0, 1)
+        add(nc.gpsimd, 0, 1, 0)
+        add(nc.gpsimd, 0, 1, 1)
+        s1(4)
+        r_v(2, 0)
+        n_c(1, 0)
+        x_c(5, 0)
+        x_c(5, 1)
+        quantise("q3", P)
+        s2("rq", ps_r, 3, 0)
+        s2("rq", ps_r, 3, 1)
+        r_v(2, 1)
+        n_c(1, 1)
+        q_c(4)
         quantise("x5", 512)
         x_t(6, 0)
-        add(nc.gpsimd, 1, 0, 0)
-        x_c(6, 1)
+        x_t(6, 1)
         s2("np", ps_n, 2, 0)
-        r_v(2, 1)
         s2("np", ps_n, 2, 1)
+        store(0, 0)
         store(0, 1)
-        s2("rq", ps_r, 3, 1)
-        n_c(2, 0)
         s1(5)
-        add(nc.gpsimd, 1, 0, 1)
-        n_c(2, 1)
-        r_v(3, 1)
+        r_v(3, 0)
+        n_c(2, 0)
         x_c(6, 0)
-        x_t(7, 0)
-        q_c(5)
-        s2("np", ps_n, 3, 1)
+        x_c(6, 1)
         quantise("q4", P)
-        add(nc.gpsimd, 1, 1, 1)
-        quantise("x6", 512)
-        x_t(7, 1)
-        n_c(3, 1)
         s2("rq", ps_r, 4, 0)
-        store(1, 0)
-        quantise("q5", P)
-        s2("np", ps_n, 4, 1)
-        r_v(4, 0)
-        x_c(7, 0)
-        s2("np", ps_n, 4, 0)
-        s2("rq", ps_r, 5, 0)
-        add(nc.gpsimd, 1, 1, 0)
-        x_c(7, 1)
-        s1(6)
-        r_v(5, 0)
-        n_c(4, 1)
-        n_c(4, 0)
-        s2("np", ps_n, 5, 0)
-        s2("rq", ps_r, 5, 1)
-        quantise("x7", 512)
-        q_c(6)
-        add(nc.gpsimd, 2, 0, 0)
-        store(1, 1)
-        s2("np", ps_n, 5, 1)
         s2("rq", ps_r, 4, 1)
-        n_c(5, 0)
-        r_v(5, 1)
-        s1(7)
-        n_c(5, 1)
-        add(nc.gpsimd, 2, 0, 1)
-        quantise("q6", P)
+        r_v(3, 1)
+        n_c(2, 1)
+        q_c(5)
+        quantise("x6", 512)
+        x_t(7, 0)
+        x_t(7, 1)
+        s2("np", ps_n, 3, 0)
+        s2("np", ps_n, 3, 1)
+        add(nc.gpsimd, 1, 0, 0)
+        add(nc.gpsimd, 1, 0, 1)
+        add(nc.gpsimd, 1, 1, 0)
+        add(nc.gpsimd, 1, 1, 1)
+        s1(6)
+        r_v(4, 0)
+        n_c(3, 0)
+        x_c(7, 0)
+        x_c(7, 1)
+        quantise("q5", P)
+        s2("rq", ps_r, 5, 0)
+        s2("rq", ps_r, 5, 1)
         r_v(4, 1)
+        n_c(3, 1)
+        q_c(6)
+        quantise("x7", 512)
+        s2("np", ps_n, 4, 0)
+        s2("np", ps_n, 4, 1)
+        store(1, 0)
+        store(1, 1)
+        s1(7)
+        r_v(5, 0)
+        n_c(4, 0)
+        quantise("q6", P)
         s2("rq", ps_r, 6, 0)
-        q_c(7)
-        s2("np", ps_n, 6, 0)
         s2("rq", ps_r, 6, 1)
-        store(2, 0)
-        n_c(6, 0)
-        quantise("q7", P)
-        s2("np", ps_n, 6, 1)
+        r_v(5, 1)
+        n_c(4, 1)
+        q_c(7)
+        s2("np", ps_n, 5, 0)
+        s2("np", ps_n, 5, 1)
+        add(nc.gpsimd, 2, 0, 0)
+        add(nc.gpsimd, 2, 0, 1)
+        add(nc.gpsimd, 2, 1, 0)
         add(nc.gpsimd, 2, 1, 1)
         r_v(6, 0)
+        n_c(5, 0)
+        quantise("q7", P)
+        s2("rq", ps_r, 7, 0)
+        s2("rq", ps_r, 7, 1)
+        r_v(6, 1)
+        n_c(5, 1)
+        s2("np", ps_n, 6, 0)
+        s2("np", ps_n, 6, 1)
+        store(2, 0)
+        store(2, 1)
+        r_v(7, 0)
+        n_c(6, 0)
+        r_v(7, 1)
         n_c(6, 1)
         s2("np", ps_n, 7, 0)
-        s2("rq", ps_r, 7, 0)
-        n_c(7, 0)
         s2("np", ps_n, 7, 1)
-        r_v(7, 0)
-        s2("rq", ps_r, 7, 1)
-        add(nc.gpsimd, 2, 1, 0)
-        n_c(7, 1)
-        r_v(6, 1)
         add(nc.gpsimd, 3, 0, 0)
-        store(2, 1)
-        r_v(7, 1)
         add(nc.gpsimd, 3, 0, 1)
         add(nc.vector, 3, 1, 0)
         add(nc.vector, 3, 1, 1)
+        n_c(7, 0)
+        n_c(7, 1)
         store(3, 0)
         store(3, 1)

@@ -11,25 +11,32 @@ FP8X4 = mybir.dt.float8_e4m3fn_x4
 MULT = mybir.AluOpType.mult
 ADD = mybir.AluOpType.add
 
-P = 128
 FLOPS = 2 * 1024 * 2048 * 512 + 2 * 1024 * 512 * 2048
 
-SCALAR_COLS = {"wd0": 176, "wd1": 176, "wd2": 176, "wd3": 176, "rq0": 176, "rq1": 176, "np0": 176, "np1": 176}
+P = 128
+PACK = 4
+BLOCKS = 8
+PASSES = 4
+CHUNK = 512
+
+SCALAR_COLS = {"wd": 256, "rq": 176, "np": 400}
+
 
 def tile_multiheadlatentattention_pa_kernel(tc, x, Wq_d, Wq_nope, Wrq, cos, sin, out):
     nc = tc.nc
     with ExitStack() as ctx:
         const = ctx.enter_context(tc.tile_pool(name="const", bufs=1))
         raw = ctx.enter_context(tc.tile_pool(name="raw", bufs=1))
-        grp = ctx.enter_context(tc.tile_pool(name="grp", bufs=3))
         mx = ctx.enter_context(tc.tile_pool(name="mx", bufs=1))
+        grp = ctx.enter_context(tc.tile_pool(name="grp", bufs=3))
         prod = ctx.enter_context(tc.tile_pool(name="prod", bufs=3))
         res = ctx.enter_context(tc.tile_pool(name="res", bufs=4))
         ps_x = ctx.enter_context(tc.psum_pool(name="ps_x", bufs=2))
         ps_q = ctx.enter_context(tc.psum_pool(name="ps_q", bufs=1))
         ps_r = ctx.enter_context(tc.psum_pool(name="ps_r", bufs=3))
         ps_n = ctx.enter_context(tc.psum_pool(name="ps_n", bufs=2))
-
+        psum_of = {"rq": ps_r, "np": ps_n}
+        tiles = {}
 
         ident = const.tile([P, P], F32, name="ident")
         make_identity(nc, ident[:])
@@ -38,26 +45,24 @@ def tile_multiheadlatentattention_pa_kernel(tc, x, Wq_d, Wq_nope, Wrq, cos, sin,
         nc.scalar.dma_start(out=cs[:, 1, :], in_=sin.rearrange("(p i) d -> p (i d)", i=4))
         ct = const.tile([P, 4, 2, 64], F32, name="ct")
 
-        tiles = {}
-        w_src = {"rq": Wrq, "np": Wq_nope}
+        def load_x(n):
+            t = raw.tile([P, 2048], BF16, name="raw_x%d" % n)
+            nc.sync.dma_start(out=t[:], in_=x[n // 4].rearrange("(p i) k -> p i k", i=4)[:, n % 4, :])
+            tiles["raw_x%d" % n] = t
 
-        def load(name):
-            if name[0] == "x":
-                n = int(name[1])
-                b, i = divmod(n, 4)
-                t = raw.tile([P, 2048], BF16, name="raw_" + name)
-                nc.sync.dma_start(out=t[:], in_=x[b].rearrange("(p i) k -> p i k", i=4)[:, i, :])
-            elif name[0] == "w":
-                g = int(name[2])
-                t = raw.tile([P, 4, 512], BF16, name="raw_" + name)
-                nc.sync.dma_start(
-                    out=t[:].rearrange("q (u e) c -> q u (e c)", u=2),
-                    in_=Wq_d[512 * g : 512 * (g + 1), :].rearrange("(u q e) c -> q u (e c)", u=2, e=2),
-                )
-            else:
-                t = raw.tile([P, 4, 1024], BF16, name="raw_" + name)
-                nc.sync.dma_start(out=t[:], in_=w_src[name].rearrange("(t p) n -> p t n", p=P))
-            tiles["raw_" + name] = t
+        def load_down(g):
+            t = raw.tile([P, PACK, CHUNK], BF16, name="raw_wd%d" % g)
+            nc.sync.dma_start(
+                out=t[:].rearrange("q (u e) c -> q u (e c)", u=2),
+                in_=Wq_d[512 * g : 512 * (g + 1), :].rearrange("(u q e) c -> q u (e c)", u=2, e=2),
+            )
+            tiles["raw_wd%d" % g] = t[:]
+
+        def load_up(kind, w):
+            t = raw.tile([P, PACK, 2 * CHUNK], BF16, name="raw_" + kind)
+            nc.sync.dma_start(out=t[:], in_=w.rearrange("(t p) n -> p t n", p=P))
+            for hg in range(2):
+                tiles["raw_%s%d" % (kind, hg)] = t[:, :, CHUNK * hg : CHUNK * (hg + 1)]
 
         def tables():
             cv = cs[:, 0, :].rearrange("p (i d) -> p i d", d=64)
@@ -66,34 +71,20 @@ def tile_multiheadlatentattention_pa_kernel(tc, x, Wq_d, Wq_nope, Wrq, cos, sin,
             nc.vector.tensor_copy(out=ct[:, :, 1, 0:32], in_=sv[:, :, 32:64])
             nc.vector.tensor_scalar_mul(out=ct[:, :, 1, 32:64], in0=sv[:, :, 0:32], scalar1=-1.0)
 
-        def get(key, pool, shape, dtype, tag):
-            if key not in tiles:
-                tiles[key] = pool.tile(shape, dtype, tag=tag, name=key, align_bytes=64)
-            return tiles[key]
-
-        def getp(key, pool, shape, tag):
-            if key not in tiles:
-                tiles[key] = pool.tile(shape, F32, tag=tag, name=key)
-            return tiles[key]
-
-        def regroup(eng, name):
-            if name[0] == "w":
-                src = tiles["raw_" + name][:]
-            else:
-                hg = int(name[2])
-                src = tiles["raw_" + name[0:2]][:, :, 512 * hg : 512 * (hg + 1)]
-            v = 512 - SCALAR_COLS[name]
-            d = get("g_" + name, grp, [P, 2048], BF16, "gw")[:].rearrange("p (c t) -> p c t", t=4)
-            if eng == "V":
-                nc.vector.tensor_copy(
-                    out=d[:, 0:v, :].rearrange("p (c i) t -> p c t i", i=4),
-                    in_=src[:, :, 0:v].rearrange("p t (c i) -> p c t i", i=4),
-                )
-            else:
-                nc.scalar.copy(
-                    out=d[:, v:512, :].rearrange("p (c i) t -> p c t i", i=4),
-                    in_=src[:, :, v:512].rearrange("p t (c i) -> p c t i", i=4),
-                )
+        def regroup(name):
+            src = tiles["raw_" + name]
+            dst = grp.tile([P, PACK * CHUNK], BF16, tag="gw", name="g_" + name, align_bytes=64)
+            tiles["g_" + name] = dst
+            d = dst[:].rearrange("p (c t) -> p c t", t=PACK)
+            v = CHUNK - SCALAR_COLS[name[0:2]]
+            nc.vector.tensor_copy(
+                out=d[:, 0:v, :].rearrange("p (c i) t -> p c t i", i=4),
+                in_=src[:, :, 0:v].rearrange("p t (c i) -> p c t i", i=4),
+            )
+            nc.scalar.copy(
+                out=d[:, v:CHUNK, :].rearrange("p (c i) t -> p c t i", i=4),
+                in_=src[:, :, v:CHUNK].rearrange("p t (c i) -> p c t i", i=4),
+            )
 
         def quantise(name, words):
             codes = mx.tile([P, words], U32, name="c_" + name, align_bytes=64)
@@ -102,25 +93,30 @@ def tile_multiheadlatentattention_pa_kernel(tc, x, Wq_d, Wq_nope, Wrq, cos, sin,
             tiles["c_" + name] = codes
             tiles["s_" + name] = scales
 
-        def x_t(n, hb):
+        def transpose_x(n):
             xw = tiles["raw_x%d" % n][:].bitcast(F32)
-            xt = getp("xt%d_%d" % (n, hb), ps_x, [P, 4, P], "xt")
-            for w in range(4):
-                c0 = P * (4 * hb + w)
-                nc.tensor.transpose(xt[:, w, :], xw[:, c0 : c0 + P], ident[:])
+            for half in range(2):
+                xt = ps_x.tile([P, 4, P], F32, tag="xt", name="xt%d_%d" % (n, half))
+                tiles["xt%d_%d" % (n, half)] = xt
+                for w in range(4):
+                    c0 = P * (4 * half + w)
+                    nc.tensor.transpose(xt[:, w, :], xw[:, c0 : c0 + P], ident[:])
 
-        def x_c(n, hb):
-            gx = get("g_x%d" % n, grp, [P, 2048], BF16, "gx")
-            gxw = gx[:].bitcast(F32).rearrange("q (g p u) -> q g p u", g=4, u=2)
-            nc.scalar.copy(
-                out=gxw[:, 2 * hb : 2 * hb + 2],
-                in_=tiles["xt%d_%d" % (n, hb)][:].rearrange("q (g u) p -> q g p u", u=2),
-            )
+        def copy_x(n):
+            gx = grp.tile([P, PASSES * P * PACK], BF16, tag="gx", name="g_x%d" % n, align_bytes=64)
+            tiles["g_x%d" % n] = gx
+            gxw = gx[:].bitcast(F32).rearrange("q (g p u) -> q g p u", g=PASSES, u=2)
+            for half in range(2):
+                nc.scalar.copy(
+                    out=gxw[:, 2 * half : 2 * half + 2],
+                    in_=tiles["xt%d_%d" % (n, half)][:].rearrange("q (g u) p -> q g p u", u=2),
+                )
 
-        def s1(n):
-            qp = getp("qp%d" % n, ps_q, [P, 4, P], "qp")
-            for j in range(4):
-                for g in range(4):
+        def stage1(n):
+            qp = ps_q.tile([P, PACK, P], F32, tag="qp", name="qp%d" % n)
+            tiles["qp%d" % n] = qp
+            for j in range(PACK):
+                for g in range(PASSES):
                     nc.tensor.matmul_mx(
                         out=qp[:, j, :],
                         lhsT=tiles["c_wd%d" % g][:, P * j : P * (j + 1)].bitcast(FP8X4),
@@ -128,18 +124,20 @@ def tile_multiheadlatentattention_pa_kernel(tc, x, Wq_d, Wq_nope, Wrq, cos, sin,
                         rhs=tiles["c_x%d" % n][:, P * g : P * (g + 1)].bitcast(FP8X4),
                         rhs_scale=tiles["s_x%d" % n][:, P * g : P * (g + 1)],
                         start=(g == 0),
-                        stop=(g == 3),
+                        stop=(g == PASSES - 1),
                     )
 
-        def q_c(n):
-            gq = get("g_q%d" % n, grp, [P, 512], BF16, "gq")
+        def copy_q(n):
+            gq = grp.tile([P, P * PACK], BF16, tag="gq", name="g_q%d" % n, align_bytes=64)
+            tiles["g_q%d" % n] = gq
             nc.scalar.copy(
-                out=gq[:].rearrange("p (n j) -> p n j", j=4),
+                out=gq[:].rearrange("p (n j) -> p n j", j=PACK),
                 in_=tiles["qp%d" % n][:].rearrange("p j n -> p n j"),
             )
 
-        def s2(kind, pool, n, hg):
-            acc = getp("%s%d_%d" % (kind, n, hg), pool, [P, 512], kind)
+        def stage2(kind, n, hg):
+            acc = psum_of[kind].tile([P, CHUNK], F32, tag=kind, name="%s%d_%d" % (kind, n, hg))
+            tiles["%s%d_%d" % (kind, n, hg)] = acc
             nc.tensor.matmul_mx(
                 out=acc[:],
                 lhsT=tiles["c_q%d" % n][:].bitcast(FP8X4),
@@ -150,8 +148,13 @@ def tile_multiheadlatentattention_pa_kernel(tc, x, Wq_d, Wq_nope, Wrq, cos, sin,
                 stop=True,
             )
 
-        def r_v(n, hg):
-            a = get("ab%d_%d" % (n // 2, hg), prod, [P, 2, 2, 512], F32, "ab")
+        def pair_tile(key, pool, shape, tag):
+            if key not in tiles:
+                tiles[key] = pool.tile(shape, F32, tag=tag, name=key)
+            return tiles[key]
+
+        def products(n, hg):
+            a = pair_tile("ab%d_%d" % (n // 2, hg), prod, [P, 2, 2, CHUNK], "ab")
             nc.vector.tensor_tensor(
                 out=a[:, n % 2].rearrange("p a (h d) -> p a h d", d=64),
                 in0=tiles["rq%d_%d" % (n, hg)][:].rearrange("p (h d) -> p h d", d=64).unsqueeze(1).to_broadcast([P, 2, 8, 64]),
@@ -159,220 +162,107 @@ def tile_multiheadlatentattention_pa_kernel(tc, x, Wq_d, Wq_nope, Wrq, cos, sin,
                 op=MULT,
             )
 
-        def n_c(n, hg):
-            o = get("ot%d_%d" % (n // 2, hg), res, [P, 8, 2, P], F32, "ot")
+        def copy_nope(n, hg):
+            o = pair_tile("ot%d_%d" % (n // 2, hg), res, [P, 8, 2, P], "ot")
             nc.scalar.copy(
                 out=o[:, :, n % 2, 64:128],
                 in_=tiles["np%d_%d" % (n, hg)][:].rearrange("p (h d) -> p h d", d=64),
             )
 
-        def add(eng, s, hg, half):
-            o = get("ot%d_%d" % (s, hg), res, [P, 8, 2, P], F32, "ot")
+        def add(s, hg, engines):
+            o = pair_tile("ot%d_%d" % (s, hg), res, [P, 8, 2, P], "ot")
             a = tiles["ab%d_%d" % (s, hg)]
-            lo = 32 * half
-            sw = 32 * (1 - half)
-            eng.tensor_tensor(
-                out=o[:, :, :, lo : lo + 32].rearrange("p h s d -> p s h d"),
-                in0=a[:, :, 0].rearrange("p s (h d) -> p s h d", d=64)[:, :, :, lo : lo + 32],
-                in1=a[:, :, 1].rearrange("p s (h d) -> p s h d", d=64)[:, :, :, sw : sw + 32],
-                op=ADD,
-            )
+            for half in range(2):
+                lo = 32 * half
+                other = 32 - lo
+                engines[half].tensor_tensor(
+                    out=o[:, :, :, lo : lo + 32].rearrange("p h s d -> p s h d"),
+                    in0=a[:, :, 0].rearrange("p s (h d) -> p s h d", d=64)[:, :, :, lo : lo + 32],
+                    in1=a[:, :, 1].rearrange("p s (h d) -> p s h d", d=64)[:, :, :, other : other + 32],
+                    op=ADD,
+                )
 
         def store(s, hg):
-            b, ip = divmod(s, 2)
             nc.sync.dma_start(
-                out=out[b, 8 * hg : 8 * hg + 8].rearrange("h (p i) d -> p h (i d)", i=4)[:, :, 256 * ip : 256 * (ip + 1)],
+                out=out[s // 2, 8 * hg : 8 * hg + 8].rearrange("h (p i) d -> p h (i d)", i=4)[:, :, 256 * (s % 2) : 256 * (s % 2 + 1)],
                 in_=tiles["ot%d_%d" % (s, hg)][:].rearrange("p h s d -> p h (s d)"),
             )
 
-        load("x0")
-        load("wd0")
-        load("wd1")
-        load("wd2")
-        load("wd3")
-        load("x1")
-        load("rq")
-        load("np")
-        load("x2")
-        load("x3")
-        load("x4")
-        load("x5")
-        load("x6")
-        load("x7")
+        load_x(0)
+        for g in range(PASSES):
+            load_down(g)
+        load_x(1)
+        load_up("rq", Wrq)
+        load_up("np", Wq_nope)
+        for n in range(2, BLOCKS):
+            load_x(n)
+
         tables()
-        x_t(0, 0)
-        x_t(0, 1)
-        x_c(0, 0)
-        x_c(0, 1)
-        regroup("V", "wd0")
-        regroup("S", "wd0")
-        quantise("x0", 512)
-        regroup("V", "wd1")
-        regroup("S", "wd1")
-        quantise("wd0", 512)
-        regroup("V", "wd2")
-        regroup("S", "wd2")
-        quantise("wd1", 512)
-        regroup("V", "wd3")
-        regroup("S", "wd3")
-        quantise("wd2", 512)
-        x_t(1, 0)
-        x_t(1, 1)
-        x_c(1, 0)
-        x_c(1, 1)
-        quantise("wd3", 512)
-        s1(0)
-        quantise("x1", 512)
-        regroup("V", "rq0")
-        regroup("S", "rq0")
-        quantise("rq0", 512)
-        regroup("V", "rq1")
-        regroup("S", "rq1")
-        q_c(0)
-        s1(1)
+        transpose_x(0)
+        copy_x(0)
+        regroup("wd0")
+        quantise("x0", CHUNK)
+        for g in range(1, PASSES):
+            regroup("wd%d" % g)
+            quantise("wd%d" % (g - 1), CHUNK)
+        transpose_x(1)
+        copy_x(1)
+        quantise("wd3", CHUNK)
+        stage1(0)
+        quantise("x1", CHUNK)
+        regroup("rq0")
+        quantise("rq0", CHUNK)
+        regroup("rq1")
+        copy_q(0)
+        stage1(1)
         quantise("q0", P)
-        quantise("rq1", 512)
-        s2("rq", ps_r, 0, 0)
-        s2("rq", ps_r, 0, 1)
-        x_t(2, 0)
-        x_t(2, 1)
-        r_v(0, 0)
-        q_c(1)
-        x_c(2, 0)
-        x_c(2, 1)
-        x_t(3, 0)
-        x_t(3, 1)
-        regroup("V", "np0")
-        regroup("S", "np0")
-        quantise("q1", P)
-        s2("rq", ps_r, 1, 0)
-        s2("rq", ps_r, 1, 1)
-        quantise("x2", 512)
-        s1(2)
-        r_v(0, 1)
-        quantise("np0", 512)
-        regroup("V", "np1")
-        regroup("S", "np1")
-        x_c(3, 0)
-        x_c(3, 1)
-        q_c(2)
-        quantise("x3", 512)
-        quantise("np1", 512)
-        x_t(4, 0)
-        x_t(4, 1)
-        s2("np", ps_n, 0, 0)
-        s2("np", ps_n, 0, 1)
-        s1(3)
-        r_v(1, 0)
-        n_c(0, 0)
-        x_c(4, 0)
-        x_c(4, 1)
-        quantise("q2", P)
-        s2("rq", ps_r, 2, 0)
-        s2("rq", ps_r, 2, 1)
-        r_v(1, 1)
-        n_c(0, 1)
-        q_c(3)
-        quantise("x4", 512)
-        x_t(5, 0)
-        x_t(5, 1)
-        s2("np", ps_n, 1, 0)
-        s2("np", ps_n, 1, 1)
-        add(nc.gpsimd, 0, 0, 0)
-        add(nc.gpsimd, 0, 0, 1)
-        add(nc.gpsimd, 0, 1, 0)
-        add(nc.gpsimd, 0, 1, 1)
-        s1(4)
-        r_v(2, 0)
-        n_c(1, 0)
-        x_c(5, 0)
-        x_c(5, 1)
-        quantise("q3", P)
-        s2("rq", ps_r, 3, 0)
-        s2("rq", ps_r, 3, 1)
-        r_v(2, 1)
-        n_c(1, 1)
-        q_c(4)
-        quantise("x5", 512)
-        x_t(6, 0)
-        x_t(6, 1)
-        s2("np", ps_n, 2, 0)
-        s2("np", ps_n, 2, 1)
-        store(0, 0)
-        store(0, 1)
-        s1(5)
-        r_v(3, 0)
-        n_c(2, 0)
-        x_c(6, 0)
-        x_c(6, 1)
-        quantise("q4", P)
-        s2("rq", ps_r, 4, 0)
-        s2("rq", ps_r, 4, 1)
-        r_v(3, 1)
-        n_c(2, 1)
-        q_c(5)
-        quantise("x6", 512)
-        x_t(7, 0)
-        x_t(7, 1)
-        s2("np", ps_n, 3, 0)
-        s2("np", ps_n, 3, 1)
-        add(nc.gpsimd, 1, 0, 0)
-        add(nc.gpsimd, 1, 0, 1)
-        add(nc.gpsimd, 1, 1, 0)
-        add(nc.gpsimd, 1, 1, 1)
-        s1(6)
-        r_v(4, 0)
-        n_c(3, 0)
-        x_c(7, 0)
-        x_c(7, 1)
-        quantise("q5", P)
-        s2("rq", ps_r, 5, 0)
-        s2("rq", ps_r, 5, 1)
-        r_v(4, 1)
-        n_c(3, 1)
-        q_c(6)
-        quantise("x7", 512)
-        s2("np", ps_n, 4, 0)
-        s2("np", ps_n, 4, 1)
-        store(1, 0)
-        store(1, 1)
-        s1(7)
-        r_v(5, 0)
-        n_c(4, 0)
-        quantise("q6", P)
-        s2("rq", ps_r, 6, 0)
-        s2("rq", ps_r, 6, 1)
-        r_v(5, 1)
-        n_c(4, 1)
-        q_c(7)
-        s2("np", ps_n, 5, 0)
-        s2("np", ps_n, 5, 1)
-        add(nc.gpsimd, 2, 0, 0)
-        add(nc.gpsimd, 2, 0, 1)
-        add(nc.gpsimd, 2, 1, 0)
-        add(nc.gpsimd, 2, 1, 1)
-        r_v(6, 0)
-        n_c(5, 0)
-        quantise("q7", P)
-        s2("rq", ps_r, 7, 0)
-        s2("rq", ps_r, 7, 1)
-        r_v(6, 1)
-        n_c(5, 1)
-        s2("np", ps_n, 6, 0)
-        s2("np", ps_n, 6, 1)
-        store(2, 0)
-        store(2, 1)
-        r_v(7, 0)
-        n_c(6, 0)
-        r_v(7, 1)
-        n_c(6, 1)
-        s2("np", ps_n, 7, 0)
-        s2("np", ps_n, 7, 1)
-        add(nc.gpsimd, 3, 0, 0)
-        add(nc.gpsimd, 3, 0, 1)
-        add(nc.vector, 3, 1, 0)
-        add(nc.vector, 3, 1, 1)
-        n_c(7, 0)
-        n_c(7, 1)
-        store(3, 0)
-        store(3, 1)
+        quantise("rq1", CHUNK)
+        stage2("rq", 0, 0)
+        stage2("rq", 0, 1)
+        transpose_x(2)
+        copy_q(1)
+        copy_x(2)
+        transpose_x(3)
+        quantise("x2", CHUNK)
+        for hg in range(2):
+            regroup("np%d" % hg)
+            quantise("np%d" % hg, CHUNK)
+
+        for n in range(BLOCKS):
+            s = n // 2
+            hg = n % 2
+            if n + 2 < BLOCKS:
+                stage1(n + 2)
+            products(2 * s, hg)
+            if n >= 1:
+                copy_nope(n - 1, 0)
+            if n + 3 < BLOCKS:
+                copy_x(n + 3)
+            if n + 1 < BLOCKS:
+                quantise("q%d" % (n + 1), P)
+                stage2("rq", n + 1, 0)
+                stage2("rq", n + 1, 1)
+            if hg == 0 and s >= 1:
+                store(s - 1, 0)
+            products(2 * s + 1, hg)
+            if n == BLOCKS - 1:
+                add(s, hg, (nc.vector, nc.vector))
+            elif n >= BLOCKS // 2:
+                add(s, hg, (nc.gpsimd, nc.vector))
+            else:
+                add(s, hg, (nc.gpsimd, nc.gpsimd))
+            if n >= 1:
+                copy_nope(n - 1, 1)
+            if n + 2 < BLOCKS:
+                copy_q(n + 2)
+            if n + 3 < BLOCKS:
+                quantise("x%d" % (n + 3), CHUNK)
+            if n + 4 < BLOCKS:
+                transpose_x(n + 4)
+            stage2("np", n, 0)
+            stage2("np", n, 1)
+            if hg == 0 and s >= 1:
+                store(s - 1, 1)
+        for hg in range(2):
+            copy_nope(BLOCKS - 1, hg)
+            store(BLOCKS // 2 - 1, hg)

@@ -19,7 +19,7 @@ BLOCKS = 8
 PASSES = 4
 CHUNK = 512
 
-SCALAR_COLS = {"wd": 256, "rq": 176, "np": 400}
+SCALAR_COLS = 176
 
 
 def tile_multiheadlatentattention_pa_kernel(tc, x, Wq_d, Wq_nope, Wrq, cos, sin, out):
@@ -76,7 +76,7 @@ def tile_multiheadlatentattention_pa_kernel(tc, x, Wq_d, Wq_nope, Wrq, cos, sin,
             dst = grp.tile([P, PACK * CHUNK], BF16, tag="gw", name="g_" + name, align_bytes=64)
             tiles["g_" + name] = dst
             d = dst[:].rearrange("p (c t) -> p c t", t=PACK)
-            v = CHUNK - SCALAR_COLS[name[0:2]]
+            v = CHUNK - SCALAR_COLS
             nc.vector.tensor_copy(
                 out=d[:, 0:v, :].rearrange("p (c i) t -> p c t i", i=4),
                 in_=src[:, :, 0:v].rearrange("p t (c i) -> p c t i", i=4),
@@ -169,13 +169,13 @@ def tile_multiheadlatentattention_pa_kernel(tc, x, Wq_d, Wq_nope, Wrq, cos, sin,
                 in_=tiles["np%d_%d" % (n, hg)][:].rearrange("p (h d) -> p h d", d=64),
             )
 
-        def add(s, hg, engines):
+        def add(eng, s, hg):
             o = pair_tile("ot%d_%d" % (s, hg), res, [P, 8, 2, P], "ot")
             a = tiles["ab%d_%d" % (s, hg)]
             for half in range(2):
                 lo = 32 * half
                 other = 32 - lo
-                engines[half].tensor_tensor(
+                eng.tensor_tensor(
                     out=o[:, :, :, lo : lo + 32].rearrange("p h s d -> p s h d"),
                     in0=a[:, :, 0].rearrange("p s (h d) -> p s h d", d=64)[:, :, :, lo : lo + 32],
                     in1=a[:, :, 1].rearrange("p s (h d) -> p s h d", d=64)[:, :, :, other : other + 32],
@@ -229,11 +229,9 @@ def tile_multiheadlatentattention_pa_kernel(tc, x, Wq_d, Wq_nope, Wrq, cos, sin,
             quantise("np%d" % hg, CHUNK)
 
         for n in range(BLOCKS):
-            s = n // 2
-            hg = n % 2
             if n + 2 < BLOCKS:
                 stage1(n + 2)
-            products(2 * s, hg)
+            products(n, 0)
             if n >= 1:
                 copy_nope(n - 1, 0)
             if n + 3 < BLOCKS:
@@ -242,15 +240,7 @@ def tile_multiheadlatentattention_pa_kernel(tc, x, Wq_d, Wq_nope, Wrq, cos, sin,
                 quantise("q%d" % (n + 1), P)
                 stage2("rq", n + 1, 0)
                 stage2("rq", n + 1, 1)
-            if hg == 0 and s >= 1:
-                store(s - 1, 0)
-            products(2 * s + 1, hg)
-            if n == BLOCKS - 1:
-                add(s, hg, (nc.vector, nc.vector))
-            elif n >= BLOCKS // 2:
-                add(s, hg, (nc.gpsimd, nc.vector))
-            else:
-                add(s, hg, (nc.gpsimd, nc.gpsimd))
+            products(n, 1)
             if n >= 1:
                 copy_nope(n - 1, 1)
             if n + 2 < BLOCKS:
@@ -261,8 +251,13 @@ def tile_multiheadlatentattention_pa_kernel(tc, x, Wq_d, Wq_nope, Wrq, cos, sin,
                 transpose_x(n + 4)
             stage2("np", n, 0)
             stage2("np", n, 1)
-            if hg == 0 and s >= 1:
-                store(s - 1, 1)
+            if n % 2 == 1:
+                add(nc.gpsimd, n // 2, 0)
+                add(nc.vector if n == BLOCKS - 1 else nc.gpsimd, n // 2, 1)
+            if n >= 2 and n % 2 == 0:
+                store(n // 2 - 1, 0)
+                store(n // 2 - 1, 1)
         for hg in range(2):
             copy_nope(BLOCKS - 1, hg)
+        for hg in range(2):
             store(BLOCKS // 2 - 1, hg)

@@ -27,8 +27,8 @@ def tile_multiheadlatentattention_pa_kernel(tc, x, Wq_d, Wq_nope, Wrq, cos, sin,
     with ExitStack() as ctx:
         const = ctx.enter_context(tc.tile_pool(name="const", bufs=1))
         raw = ctx.enter_context(tc.tile_pool(name="raw", bufs=1))
+        grp = ctx.enter_context(tc.tile_pool(name="grp", bufs=4))
         mx = ctx.enter_context(tc.tile_pool(name="mx", bufs=1))
-        grp = ctx.enter_context(tc.tile_pool(name="grp", bufs=3))
         prod = ctx.enter_context(tc.tile_pool(name="prod", bufs=3))
         res = ctx.enter_context(tc.tile_pool(name="res", bufs=4))
         ps_x = ctx.enter_context(tc.psum_pool(name="ps_x", bufs=2))
@@ -150,7 +150,7 @@ def tile_multiheadlatentattention_pa_kernel(tc, x, Wq_d, Wq_nope, Wrq, cos, sin,
 
         def pair_tile(key, pool, shape, tag):
             if key not in tiles:
-                tiles[key] = pool.tile(shape, F32, tag=tag, name=key)
+                tiles[key] = pool.tile(shape, F32, tag=tag, name=key, align_bytes=64)
             return tiles[key]
 
         def products(n, hg):
@@ -188,6 +188,20 @@ def tile_multiheadlatentattention_pa_kernel(tc, x, Wq_d, Wq_nope, Wrq, cos, sin,
                 in_=tiles["ot%d_%d" % (s, hg)][:].rearrange("p h s d -> p h (s d)"),
             )
 
+        def quantised_x(n):
+            transpose_x(n)
+            copy_x(n)
+            quantise("x%d" % n, CHUNK)
+
+        def quantised_latent(n):
+            stage1(n)
+            copy_q(n)
+            quantise("q%d" % n, P)
+
+        def weight(name):
+            regroup(name)
+            quantise(name, CHUNK)
+
         load_x(0)
         for g in range(PASSES):
             load_down(g)
@@ -198,66 +212,33 @@ def tile_multiheadlatentattention_pa_kernel(tc, x, Wq_d, Wq_nope, Wrq, cos, sin,
             load_x(n)
 
         tables()
-        transpose_x(0)
-        copy_x(0)
-        regroup("wd0")
-        quantise("x0", CHUNK)
-        for g in range(1, PASSES):
-            regroup("wd%d" % g)
-            quantise("wd%d" % (g - 1), CHUNK)
-        transpose_x(1)
-        copy_x(1)
-        quantise("wd3", CHUNK)
-        stage1(0)
-        quantise("x1", CHUNK)
-        regroup("rq0")
-        quantise("rq0", CHUNK)
-        regroup("rq1")
-        copy_q(0)
-        stage1(1)
-        quantise("q0", P)
-        quantise("rq1", CHUNK)
-        stage2("rq", 0, 0)
-        stage2("rq", 0, 1)
-        transpose_x(2)
-        copy_q(1)
-        copy_x(2)
-        transpose_x(3)
-        quantise("x2", CHUNK)
-        for hg in range(2):
-            regroup("np%d" % hg)
-            quantise("np%d" % hg, CHUNK)
+        quantised_x(0)
+        for g in range(PASSES):
+            weight("wd%d" % g)
+        quantised_latent(0)
+        quantised_x(1)
+        quantised_latent(1)
 
-        for n in range(BLOCKS):
-            if n + 2 < BLOCKS:
-                stage1(n + 2)
-            products(n, 0)
-            if n >= 1:
-                copy_nope(n - 1, 0)
-            if n + 3 < BLOCKS:
-                copy_x(n + 3)
-            if n + 1 < BLOCKS:
-                quantise("q%d" % (n + 1), P)
-                stage2("rq", n + 1, 0)
-                stage2("rq", n + 1, 1)
-            products(n, 1)
-            if n >= 1:
-                copy_nope(n - 1, 1)
-            if n + 2 < BLOCKS:
-                copy_q(n + 2)
-            if n + 3 < BLOCKS:
-                quantise("x%d" % (n + 3), CHUNK)
-            if n + 4 < BLOCKS:
-                transpose_x(n + 4)
-            stage2("np", n, 0)
-            stage2("np", n, 1)
-            if n % 2 == 1:
-                add(nc.gpsimd, n // 2, 0)
-                add(nc.vector if n == BLOCKS - 1 else nc.gpsimd, n // 2, 1)
-            if n >= 2 and n % 2 == 0:
-                store(n // 2 - 1, 0)
-                store(n // 2 - 1, 1)
-        for hg in range(2):
-            copy_nope(BLOCKS - 1, hg)
-        for hg in range(2):
-            store(BLOCKS // 2 - 1, hg)
+        for s in range(BLOCKS // 2):
+            pair = (2 * s, 2 * s + 1)
+            following = [n + 2 for n in pair if n + 2 < BLOCKS]
+            for n in following:
+                quantised_x(n)
+            for hg in range(2):
+                if hg == 1:
+                    for n in following:
+                        quantised_latent(n)
+                if s == 0:
+                    weight("rq%d" % hg)
+                for n in pair:
+                    stage2("rq", n, hg)
+                for n in pair:
+                    products(n, hg)
+                add(nc.vector if s == BLOCKS // 2 - 1 else nc.gpsimd, s, hg)
+                if s == 0:
+                    weight("np%d" % hg)
+                for n in pair:
+                    stage2("np", n, hg)
+                for n in pair:
+                    copy_nope(n, hg)
+                store(s, hg)

@@ -27,7 +27,7 @@ def tile_multiheadlatentattention_pa_kernel(tc, x, Wq_d, Wq_nope, Wrq, cos, sin,
     with ExitStack() as ctx:
         const = ctx.enter_context(tc.tile_pool(name="const", bufs=1))
         raw = ctx.enter_context(tc.tile_pool(name="raw", bufs=1))
-        grp = ctx.enter_context(tc.tile_pool(name="grp", bufs=4))
+        grp = ctx.enter_context(tc.tile_pool(name="grp", bufs=3))
         mx = ctx.enter_context(tc.tile_pool(name="mx", bufs=1))
         prod = ctx.enter_context(tc.tile_pool(name="prod", bufs=3))
         res = ctx.enter_context(tc.tile_pool(name="res", bufs=4))
@@ -37,6 +37,7 @@ def tile_multiheadlatentattention_pa_kernel(tc, x, Wq_d, Wq_nope, Wrq, cos, sin,
         ps_n = ctx.enter_context(tc.psum_pool(name="ps_n", bufs=2))
         psum_of = {"rq": ps_r, "np": ps_n}
         tiles = {}
+        ctx.enter_context(tc.manual_schedule())
 
         ident = const.tile([P, P], F32, name="ident")
         make_identity(nc, ident[:])
@@ -188,20 +189,6 @@ def tile_multiheadlatentattention_pa_kernel(tc, x, Wq_d, Wq_nope, Wrq, cos, sin,
                 in_=tiles["ot%d_%d" % (s, hg)][:].rearrange("p h s d -> p h (s d)"),
             )
 
-        def quantised_x(n):
-            transpose_x(n)
-            copy_x(n)
-            quantise("x%d" % n, CHUNK)
-
-        def quantised_latent(n):
-            stage1(n)
-            copy_q(n)
-            quantise("q%d" % n, P)
-
-        def weight(name):
-            regroup(name)
-            quantise(name, CHUNK)
-
         load_x(0)
         for g in range(PASSES):
             load_down(g)
@@ -212,33 +199,73 @@ def tile_multiheadlatentattention_pa_kernel(tc, x, Wq_d, Wq_nope, Wrq, cos, sin,
             load_x(n)
 
         tables()
-        quantised_x(0)
-        for g in range(PASSES):
-            weight("wd%d" % g)
-        quantised_latent(0)
-        quantised_x(1)
-        quantised_latent(1)
+        transpose_x(0)
+        copy_x(0)
+        regroup("wd0")
+        quantise("x0", CHUNK)
+        for g in range(1, PASSES):
+            regroup("wd%d" % g)
+            quantise("wd%d" % (g - 1), CHUNK)
+        transpose_x(1)
+        copy_x(1)
+        quantise("wd3", CHUNK)
+        stage1(0)
+        quantise("x1", CHUNK)
+        regroup("rq0")
+        quantise("rq0", CHUNK)
+        regroup("rq1")
+        copy_q(0)
+        stage1(1)
+        quantise("q0", P)
+        quantise("rq1", CHUNK)
+        stage2("rq", 0, 0)
+        stage2("rq", 0, 1)
+        transpose_x(2)
 
-        for s in range(BLOCKS // 2):
-            pair = (2 * s, 2 * s + 1)
-            following = [n + 2 for n in pair if n + 2 < BLOCKS]
-            for n in following:
-                quantised_x(n)
-            for hg in range(2):
-                if hg == 1:
-                    for n in following:
-                        quantised_latent(n)
-                if s == 0:
-                    weight("rq%d" % hg)
-                for n in pair:
-                    stage2("rq", n, hg)
-                for n in pair:
-                    products(n, hg)
-                add(nc.vector if s == BLOCKS // 2 - 1 else nc.gpsimd, s, hg)
-                if s == 0:
-                    weight("np%d" % hg)
-                for n in pair:
-                    stage2("np", n, hg)
-                for n in pair:
-                    copy_nope(n, hg)
-                store(s, hg)
+        for n in range(BLOCKS):
+            if 1 <= n < BLOCKS - 2:
+                stage1(n + 2)
+            products(n, 0)
+            if n == 0:
+                copy_q(1)
+                copy_x(2)
+                transpose_x(3)
+                regroup("np0")
+            else:
+                copy_nope(n - 1, 0)
+                if n + 3 < BLOCKS:
+                    copy_x(n + 3)
+            if n + 1 < BLOCKS:
+                quantise("q%d" % (n + 1), P)
+                stage2("rq", n + 1, 0)
+                stage2("rq", n + 1, 1)
+            if n == 0:
+                quantise("x2", CHUNK)
+                stage1(2)
+            products(n, 1)
+            if n == 0:
+                quantise("np0", CHUNK)
+                regroup("np1")
+                copy_x(3)
+            else:
+                copy_nope(n - 1, 1)
+            if n + 2 < BLOCKS:
+                copy_q(n + 2)
+            if n + 3 < BLOCKS:
+                quantise("x%d" % (n + 3), CHUNK)
+            if n == 0:
+                quantise("np1", CHUNK)
+            if n + 4 < BLOCKS:
+                transpose_x(n + 4)
+            stage2("np", n, 0)
+            stage2("np", n, 1)
+            if n % 2 == 1:
+                add(nc.gpsimd, n // 2, 0)
+                add(nc.vector if n == BLOCKS - 1 else nc.gpsimd, n // 2, 1)
+            if n >= 2 and n % 2 == 0:
+                store(n // 2 - 1, 0)
+                store(n // 2 - 1, 1)
+        for hg in range(2):
+            copy_nope(BLOCKS - 1, hg)
+        for hg in range(2):
+            store(BLOCKS // 2 - 1, hg)

@@ -15,9 +15,13 @@ FLOPS = 2 * 1024 * 2048 * 512 + 2 * 1024 * 512 * 2048
 
 P = 128
 PACK = 4
-BLOCKS = 8
+HIDDEN = 2048
 PASSES = 4
+BLOCKS = 8
 CHUNK = 512
+GROUP = 8
+ROT = 64
+HALF = 32
 
 SCALAR_COLS = 176
 
@@ -41,50 +45,50 @@ def tile_multiheadlatentattention_pa_kernel(tc, x, Wq_d, Wq_nope, Wrq, cos, sin,
 
         ident = const.tile([P, P], F32, name="ident")
         make_identity(nc, ident[:])
-        cs = const.tile([P, 2, 256], BF16, name="cs")
+        cs = const.tile([P, 2, 4 * ROT], BF16, name="cs")
         nc.scalar.dma_start(out=cs[:, 0, :], in_=cos.rearrange("(p i) d -> p (i d)", i=4))
         nc.scalar.dma_start(out=cs[:, 1, :], in_=sin.rearrange("(p i) d -> p (i d)", i=4))
-        ct = const.tile([P, 4, 2, 64], F32, name="ct")
+        factors = const.tile([P, 4, 2, ROT], F32, name="ct")
 
         def load_x(n):
-            t = raw.tile([P, 2048], BF16, name="raw_x%d" % n)
-            nc.sync.dma_start(out=t[:], in_=x[n // 4].rearrange("(p i) k -> p i k", i=4)[:, n % 4, :])
-            tiles["raw_x%d" % n] = t
+            dst = raw.tile([P, HIDDEN], BF16, name="raw_x%d" % n)
+            nc.sync.dma_start(out=dst[:], in_=x[n // 4].rearrange("(p i) k -> p i k", i=4)[:, n % 4, :])
+            tiles["raw_x%d" % n] = dst
 
         def load_down(g):
-            t = raw.tile([P, PACK, CHUNK], BF16, name="raw_wd%d" % g)
+            dst = raw.tile([P, PACK, CHUNK], BF16, name="raw_wd%d" % g)
             nc.sync.dma_start(
-                out=t[:].rearrange("q (u e) c -> q u (e c)", u=2),
+                out=dst[:].rearrange("q (u e) c -> q u (e c)", u=2),
                 in_=Wq_d[512 * g : 512 * (g + 1), :].rearrange("(u q e) c -> q u (e c)", u=2, e=2),
             )
-            tiles["raw_wd%d" % g] = t[:]
+            tiles["raw_wd%d" % g] = dst[:]
 
-        def load_up(kind, w):
-            t = raw.tile([P, PACK, 2 * CHUNK], BF16, name="raw_" + kind)
-            nc.sync.dma_start(out=t[:], in_=w.rearrange("(t p) n -> p t n", p=P))
+        def load_up(kind, weight):
+            dst = raw.tile([P, PACK, 2 * CHUNK], BF16, name="raw_" + kind)
+            nc.sync.dma_start(out=dst[:], in_=weight.rearrange("(j p) c -> p j c", p=P))
             for hg in range(2):
-                tiles["raw_%s%d" % (kind, hg)] = t[:, :, CHUNK * hg : CHUNK * (hg + 1)]
+                tiles["raw_%s%d" % (kind, hg)] = dst[:, :, CHUNK * hg : CHUNK * (hg + 1)]
 
         def tables():
-            cv = cs[:, 0, :].rearrange("p (i d) -> p i d", d=64)
-            sv = cs[:, 1, :].rearrange("p (i d) -> p i d", d=64)
-            nc.vector.tensor_copy(out=ct[:, :, 0, :], in_=cv)
-            nc.vector.tensor_copy(out=ct[:, :, 1, 0:32], in_=sv[:, :, 32:64])
-            nc.vector.tensor_scalar_mul(out=ct[:, :, 1, 32:64], in0=sv[:, :, 0:32], scalar1=-1.0)
+            cos_v = cs[:, 0, :].rearrange("p (i d) -> p i d", d=ROT)
+            sin_v = cs[:, 1, :].rearrange("p (i d) -> p i d", d=ROT)
+            nc.vector.tensor_copy(out=factors[:, :, 0, :], in_=cos_v)
+            nc.vector.tensor_copy(out=factors[:, :, 1, 0:HALF], in_=sin_v[:, :, HALF:ROT])
+            nc.vector.tensor_scalar_mul(out=factors[:, :, 1, HALF:ROT], in0=sin_v[:, :, 0:HALF], scalar1=-1.0)
 
         def regroup(name):
             src = tiles["raw_" + name]
             dst = grp.tile([P, PACK * CHUNK], BF16, tag="gw", name="g_" + name, align_bytes=64)
             tiles["g_" + name] = dst
-            d = dst[:].rearrange("p (c t) -> p c t", t=PACK)
-            v = CHUNK - SCALAR_COLS
+            view = dst[:].rearrange("p (c j) -> p c j", j=PACK)
+            cut = CHUNK - SCALAR_COLS
             nc.vector.tensor_copy(
-                out=d[:, 0:v, :].rearrange("p (c i) t -> p c t i", i=4),
-                in_=src[:, :, 0:v].rearrange("p t (c i) -> p c t i", i=4),
+                out=view[:, 0:cut, :].rearrange("p (c r) j -> p c j r", r=4),
+                in_=src[:, :, 0:cut].rearrange("p j (c r) -> p c j r", r=4),
             )
             nc.scalar.copy(
-                out=d[:, v:CHUNK, :].rearrange("p (c i) t -> p c t i", i=4),
-                in_=src[:, :, v:CHUNK].rearrange("p t (c i) -> p c t i", i=4),
+                out=view[:, cut:CHUNK, :].rearrange("p (c r) j -> p c j r", r=4),
+                in_=src[:, :, cut:CHUNK].rearrange("p j (c r) -> p c j r", r=4),
             )
 
         def quantise(name, words):
@@ -95,22 +99,22 @@ def tile_multiheadlatentattention_pa_kernel(tc, x, Wq_d, Wq_nope, Wrq, cos, sin,
             tiles["s_" + name] = scales
 
         def transpose_x(n):
-            xw = tiles["raw_x%d" % n][:].bitcast(F32)
-            for half in range(2):
-                xt = ps_x.tile([P, 4, P], F32, tag="xt", name="xt%d_%d" % (n, half))
-                tiles["xt%d_%d" % (n, half)] = xt
-                for w in range(4):
-                    c0 = P * (4 * half + w)
-                    nc.tensor.transpose(xt[:, w, :], xw[:, c0 : c0 + P], ident[:])
+            words = tiles["raw_x%d" % n][:].bitcast(F32)
+            for bank in range(2):
+                xt = ps_x.tile([P, 4, P], F32, tag="xt", name="xt%d_%d" % (n, bank))
+                tiles["xt%d_%d" % (n, bank)] = xt
+                for quarter in range(4):
+                    first = P * (4 * bank + quarter)
+                    nc.tensor.transpose(xt[:, quarter, :], words[:, first : first + P], ident[:])
 
         def copy_x(n):
             gx = grp.tile([P, PASSES * P * PACK], BF16, tag="gx", name="g_x%d" % n, align_bytes=64)
             tiles["g_x%d" % n] = gx
-            gxw = gx[:].bitcast(F32).rearrange("q (g p u) -> q g p u", g=PASSES, u=2)
-            for half in range(2):
+            view = gx[:].bitcast(F32).rearrange("q (g m u) -> q g m u", g=PASSES, u=2)
+            for bank in range(2):
                 nc.scalar.copy(
-                    out=gxw[:, 2 * half : 2 * half + 2],
-                    in_=tiles["xt%d_%d" % (n, half)][:].rearrange("q (g u) p -> q g p u", u=2),
+                    out=view[:, 2 * bank : 2 * bank + 2],
+                    in_=tiles["xt%d_%d" % (n, bank)][:].rearrange("q (g u) m -> q g m u", u=2),
                 )
 
         def stage1(n):
@@ -132,8 +136,8 @@ def tile_multiheadlatentattention_pa_kernel(tc, x, Wq_d, Wq_nope, Wrq, cos, sin,
             gq = grp.tile([P, P * PACK], BF16, tag="gq", name="g_q%d" % n, align_bytes=64)
             tiles["g_q%d" % n] = gq
             nc.scalar.copy(
-                out=gq[:].rearrange("p (n j) -> p n j", j=PACK),
-                in_=tiles["qp%d" % n][:].rearrange("p j n -> p n j"),
+                out=gq[:].rearrange("p (m j) -> p m j", j=PACK),
+                in_=tiles["qp%d" % n][:].rearrange("p j m -> p m j"),
             )
 
         def stage2(kind, n, hg):
@@ -155,38 +159,42 @@ def tile_multiheadlatentattention_pa_kernel(tc, x, Wq_d, Wq_nope, Wrq, cos, sin,
             return tiles[key]
 
         def products(n, hg):
-            a = pair_tile("ab%d_%d" % (n // 2, hg), prod, [P, 2, 2, CHUNK], "ab")
+            both = pair_tile("ab%d_%d" % (n // 2, hg), prod, [P, 2, 2, CHUNK], "ab")
+            shape = [P, 2, GROUP, ROT]
             nc.vector.tensor_tensor(
-                out=a[:, n % 2].rearrange("p a (h d) -> p a h d", d=64),
-                in0=tiles["rq%d_%d" % (n, hg)][:].rearrange("p (h d) -> p h d", d=64).unsqueeze(1).to_broadcast([P, 2, 8, 64]),
-                in1=ct[:, n % 4].unsqueeze(2).to_broadcast([P, 2, 8, 64]),
+                out=both[:, n % 2].rearrange("p f (h d) -> p f h d", d=ROT),
+                in0=tiles["rq%d_%d" % (n, hg)][:].rearrange("p (h d) -> p h d", d=ROT).unsqueeze(1).to_broadcast(shape),
+                in1=factors[:, n % 4].unsqueeze(2).to_broadcast(shape),
                 op=MULT,
             )
 
         def copy_nope(n, hg):
-            o = pair_tile("ot%d_%d" % (n // 2, hg), res, [P, 8, 2, P], "ot")
+            done = pair_tile("ot%d_%d" % (n // 2, hg), res, [P, GROUP, 2, 2 * ROT], "ot")
             nc.scalar.copy(
-                out=o[:, :, n % 2, 64:128],
-                in_=tiles["np%d_%d" % (n, hg)][:].rearrange("p (h d) -> p h d", d=64),
+                out=done[:, :, n % 2, ROT : 2 * ROT],
+                in_=tiles["np%d_%d" % (n, hg)][:].rearrange("p (h d) -> p h d", d=ROT),
             )
 
-        def add(eng, s, hg):
-            o = pair_tile("ot%d_%d" % (s, hg), res, [P, 8, 2, P], "ot")
-            a = tiles["ab%d_%d" % (s, hg)]
+        def add(eng, pair, hg):
+            done = pair_tile("ot%d_%d" % (pair, hg), res, [P, GROUP, 2, 2 * ROT], "ot")
+            both = tiles["ab%d_%d" % (pair, hg)]
             for half in range(2):
-                lo = 32 * half
-                other = 32 - lo
+                own = HALF * half
+                other = HALF - own
                 eng.tensor_tensor(
-                    out=o[:, :, :, lo : lo + 32].rearrange("p h s d -> p s h d"),
-                    in0=a[:, :, 0].rearrange("p s (h d) -> p s h d", d=64)[:, :, :, lo : lo + 32],
-                    in1=a[:, :, 1].rearrange("p s (h d) -> p s h d", d=64)[:, :, :, other : other + 32],
+                    out=done[:, :, :, own : own + HALF].rearrange("p h b d -> p b h d"),
+                    in0=both[:, :, 0].rearrange("p b (h d) -> p b h d", d=ROT)[:, :, :, own : own + HALF],
+                    in1=both[:, :, 1].rearrange("p b (h d) -> p b h d", d=ROT)[:, :, :, other : other + HALF],
                     op=ADD,
                 )
 
-        def store(s, hg):
+        def store(pair, hg):
+            run = 2 * 2 * ROT
             nc.sync.dma_start(
-                out=out[s // 2, 8 * hg : 8 * hg + 8].rearrange("h (p i) d -> p h (i d)", i=4)[:, :, 256 * (s % 2) : 256 * (s % 2 + 1)],
-                in_=tiles["ot%d_%d" % (s, hg)][:].rearrange("p h s d -> p h (s d)"),
+                out=out[pair // 2, GROUP * hg : GROUP * hg + GROUP].rearrange("h (p i) d -> p h (i d)", i=4)[
+                    :, :, run * (pair % 2) : run * (pair % 2 + 1)
+                ],
+                in_=tiles["ot%d_%d" % (pair, hg)][:].rearrange("p h b d -> p h (b d)"),
             )
 
         load_x(0)
@@ -198,74 +206,75 @@ def tile_multiheadlatentattention_pa_kernel(tc, x, Wq_d, Wq_nope, Wrq, cos, sin,
         for n in range(2, BLOCKS):
             load_x(n)
 
+        def weight(name):
+            regroup(name)
+            quantise(name, CHUNK)
+
         tables()
-        transpose_x(0)
-        copy_x(0)
         regroup("wd0")
-        quantise("x0", CHUNK)
         for g in range(1, PASSES):
             regroup("wd%d" % g)
             quantise("wd%d" % (g - 1), CHUNK)
-        transpose_x(1)
-        copy_x(1)
         quantise("wd3", CHUNK)
+        transpose_x(0)
+        copy_x(0)
+        quantise("x0", CHUNK)
+        transpose_x(1)
+        weight("rq0")
+        weight("rq1")
         stage1(0)
+        copy_x(1)
         quantise("x1", CHUNK)
-        regroup("rq0")
-        quantise("rq0", CHUNK)
-        regroup("rq1")
         copy_q(0)
-        stage1(1)
+        weight("np0")
+        transpose_x(2)
         quantise("q0", P)
-        quantise("rq1", CHUNK)
+        stage1(1)
+        weight("np1")
+        copy_x(2)
         stage2("rq", 0, 0)
         stage2("rq", 0, 1)
-        transpose_x(2)
+        quantise("x2", CHUNK)
+        copy_q(1)
+        transpose_x(3)
 
-        for n in range(BLOCKS):
-            if 1 <= n < BLOCKS - 2:
-                stage1(n + 2)
-            products(n, 0)
-            if n == 0:
-                copy_q(1)
-                copy_x(2)
-                transpose_x(3)
-                regroup("np0")
-            else:
+        def live(m):
+            return 0 <= m < BLOCKS
+
+        for n in range(BLOCKS + 1):
+            pair_rotated = live(n) and n % 2 == 1
+            pair_copied = live(n - 1) and (n - 1) % 2 == 1
+            if live(n):
+                products(n, 0)
+            if pair_rotated:
+                add(nc.gpsimd, n // 2, 0)
+            if live(n - 1):
                 copy_nope(n - 1, 0)
-                if n + 3 < BLOCKS:
-                    copy_x(n + 3)
-            if n + 1 < BLOCKS:
+            if live(n + 1):
                 quantise("q%d" % (n + 1), P)
+            if pair_copied:
+                store((n - 1) // 2, 0)
+            if live(n + 2):
+                stage1(n + 2)
+            if live(n):
+                products(n, 1)
+            if live(n + 3):
+                copy_x(n + 3)
+            if live(n - 1):
+                copy_nope(n - 1, 1)
+            if live(n + 1):
                 stage2("rq", n + 1, 0)
                 stage2("rq", n + 1, 1)
-            if n == 0:
-                quantise("x2", CHUNK)
-                stage1(2)
-            products(n, 1)
-            if n == 0:
-                quantise("np0", CHUNK)
-                regroup("np1")
-                copy_x(3)
-            else:
-                copy_nope(n - 1, 1)
-            if n + 2 < BLOCKS:
-                copy_q(n + 2)
-            if n + 3 < BLOCKS:
-                quantise("x%d" % (n + 3), CHUNK)
-            if n == 0:
-                quantise("np1", CHUNK)
-            if n + 4 < BLOCKS:
-                transpose_x(n + 4)
-            stage2("np", n, 0)
-            stage2("np", n, 1)
-            if n % 2 == 1:
-                add(nc.gpsimd, n // 2, 0)
+            if pair_rotated:
                 add(nc.vector if n == BLOCKS - 1 else nc.gpsimd, n // 2, 1)
-            if n >= 2 and n % 2 == 0:
-                store(n // 2 - 1, 0)
-                store(n // 2 - 1, 1)
-        for hg in range(2):
-            copy_nope(BLOCKS - 1, hg)
-        for hg in range(2):
-            store(BLOCKS // 2 - 1, hg)
+            if live(n + 3):
+                quantise("x%d" % (n + 3), CHUNK)
+            if live(n):
+                stage2("np", n, 0)
+                stage2("np", n, 1)
+            if live(n + 2):
+                copy_q(n + 2)
+            if pair_copied:
+                store((n - 1) // 2, 1)
+            if live(n + 4):
+                transpose_x(n + 4)

@@ -23,7 +23,7 @@ GROUP = 8
 ROT = 64
 HALF = 32
 
-SCALAR_COLS = 176
+SCALAR_COLS = {"wd": 256, "rq": 176, "np": 400}
 
 
 def tile_multiheadlatentattention_pa_kernel(tc, x, Wq_d, Wq_nope, Wrq, cos, sin, out):
@@ -41,7 +41,6 @@ def tile_multiheadlatentattention_pa_kernel(tc, x, Wq_d, Wq_nope, Wrq, cos, sin,
         ps_n = ctx.enter_context(tc.psum_pool(name="ps_n", bufs=2))
         psum_of = {"rq": ps_r, "np": ps_n}
         tiles = {}
-        ctx.enter_context(tc.manual_schedule())
 
         ident = const.tile([P, P], F32, name="ident")
         make_identity(nc, ident[:])
@@ -81,7 +80,7 @@ def tile_multiheadlatentattention_pa_kernel(tc, x, Wq_d, Wq_nope, Wrq, cos, sin,
             dst = grp.tile([P, PACK * CHUNK], BF16, tag="gw", name="g_" + name, align_bytes=64)
             tiles["g_" + name] = dst
             view = dst[:].rearrange("p (c j) -> p c j", j=PACK)
-            cut = CHUNK - SCALAR_COLS
+            cut = CHUNK - SCALAR_COLS[name[0:2]]
             nc.vector.tensor_copy(
                 out=view[:, 0:cut, :].rearrange("p (c r) j -> p c j r", r=4),
                 in_=src[:, :, 0:cut].rearrange("p j (c r) -> p c j r", r=4),
@@ -206,75 +205,74 @@ def tile_multiheadlatentattention_pa_kernel(tc, x, Wq_d, Wq_nope, Wrq, cos, sin,
         for n in range(2, BLOCKS):
             load_x(n)
 
-        def weight(name):
-            regroup(name)
-            quantise(name, CHUNK)
-
         tables()
+        transpose_x(0)
+        copy_x(0)
         regroup("wd0")
+        quantise("x0", CHUNK)
         for g in range(1, PASSES):
             regroup("wd%d" % g)
             quantise("wd%d" % (g - 1), CHUNK)
-        quantise("wd3", CHUNK)
-        transpose_x(0)
-        copy_x(0)
-        quantise("x0", CHUNK)
         transpose_x(1)
-        weight("rq0")
-        weight("rq1")
-        stage1(0)
         copy_x(1)
+        quantise("wd3", CHUNK)
+        stage1(0)
         quantise("x1", CHUNK)
+        regroup("rq0")
+        quantise("rq0", CHUNK)
+        regroup("rq1")
         copy_q(0)
-        weight("np0")
-        transpose_x(2)
-        quantise("q0", P)
         stage1(1)
-        weight("np1")
-        copy_x(2)
+        quantise("q0", P)
+        quantise("rq1", CHUNK)
         stage2("rq", 0, 0)
         stage2("rq", 0, 1)
-        quantise("x2", CHUNK)
-        copy_q(1)
-        transpose_x(3)
+        transpose_x(2)
 
-        def live(m):
-            return 0 <= m < BLOCKS
-
-        for n in range(BLOCKS + 1):
-            pair_rotated = live(n) and n % 2 == 1
-            pair_copied = live(n - 1) and (n - 1) % 2 == 1
-            if live(n):
-                products(n, 0)
-            if pair_rotated:
-                add(nc.gpsimd, n // 2, 0)
-            if live(n - 1):
-                copy_nope(n - 1, 0)
-            if live(n + 1):
-                quantise("q%d" % (n + 1), P)
-            if pair_copied:
-                store((n - 1) // 2, 0)
-            if live(n + 2):
+        for n in range(BLOCKS):
+            if 1 <= n < BLOCKS - 2:
                 stage1(n + 2)
-            if live(n):
-                products(n, 1)
-            if live(n + 3):
-                copy_x(n + 3)
-            if live(n - 1):
-                copy_nope(n - 1, 1)
-            if live(n + 1):
+            products(n, 0)
+            if n == 0:
+                copy_q(1)
+                copy_x(2)
+                transpose_x(3)
+                regroup("np0")
+            else:
+                copy_nope(n - 1, 0)
+                if n + 3 < BLOCKS:
+                    copy_x(n + 3)
+            if n + 1 < BLOCKS:
+                quantise("q%d" % (n + 1), P)
                 stage2("rq", n + 1, 0)
                 stage2("rq", n + 1, 1)
-            if pair_rotated:
-                add(nc.vector if n == BLOCKS - 1 else nc.gpsimd, n // 2, 1)
-            if live(n + 3):
-                quantise("x%d" % (n + 3), CHUNK)
-            if live(n):
-                stage2("np", n, 0)
-                stage2("np", n, 1)
-            if live(n + 2):
+            if n == 0:
+                quantise("x2", CHUNK)
+                stage1(2)
+            products(n, 1)
+            if n == 0:
+                quantise("np0", CHUNK)
+                regroup("np1")
+                copy_x(3)
+            else:
+                copy_nope(n - 1, 1)
+            if n + 2 < BLOCKS:
                 copy_q(n + 2)
-            if pair_copied:
-                store((n - 1) // 2, 1)
-            if live(n + 4):
+            if n + 3 < BLOCKS:
+                quantise("x%d" % (n + 3), CHUNK)
+            if n == 0:
+                quantise("np1", CHUNK)
+            if n + 4 < BLOCKS:
                 transpose_x(n + 4)
+            stage2("np", n, 0)
+            stage2("np", n, 1)
+            if n % 2 == 1:
+                add(nc.gpsimd, n // 2, 0)
+                add(nc.vector if n == BLOCKS - 1 else nc.gpsimd, n // 2, 1)
+            if n >= 2 and n % 2 == 0:
+                store(n // 2 - 1, 0)
+                store(n // 2 - 1, 1)
+        for hg in range(2):
+            copy_nope(BLOCKS - 1, hg)
+        for hg in range(2):
+            store(BLOCKS // 2 - 1, hg)

from contextlib import ExitStack

import concourse.mybir as mybir
from concourse.masks import make_identity

F32 = mybir.dt.float32
BF16 = mybir.dt.bfloat16
U32 = mybir.dt.uint32
U8 = mybir.dt.uint8
FP8X4 = mybir.dt.float8_e4m3fn_x4
MULT = mybir.AluOpType.mult
ADD = mybir.AluOpType.add

FLOPS = 2 * 1024 * 2048 * 512 + 2 * 1024 * 512 * 2048

P = 128
PACK = 4
HIDDEN = 2048
PASSES = 4
BLOCKS = 8
CHUNK = 512
GROUP = 8
ROT = 64
HALF = 32

SCALAR_COLS = {"wd": 256, "rq": 176, "np": 400}


def tile_multiheadlatentattention_pa_kernel(tc, x, Wq_d, Wq_nope, Wrq, cos, sin, out):
    nc = tc.nc
    with ExitStack() as ctx:
        const = ctx.enter_context(tc.tile_pool(name="const", bufs=1))
        raw = ctx.enter_context(tc.tile_pool(name="raw", bufs=1))
        grp = ctx.enter_context(tc.tile_pool(name="grp", bufs=3))
        mx = ctx.enter_context(tc.tile_pool(name="mx", bufs=1))
        prod = ctx.enter_context(tc.tile_pool(name="prod", bufs=3))
        res = ctx.enter_context(tc.tile_pool(name="res", bufs=4))
        ps_x = ctx.enter_context(tc.psum_pool(name="ps_x", bufs=2))
        ps_q = ctx.enter_context(tc.psum_pool(name="ps_q", bufs=1))
        ps_r = ctx.enter_context(tc.psum_pool(name="ps_r", bufs=3))
        ps_n = ctx.enter_context(tc.psum_pool(name="ps_n", bufs=2))
        psum_of = {"rq": ps_r, "np": ps_n}
        tiles = {}

        ident = const.tile([P, P], F32, name="ident")
        make_identity(nc, ident[:])
        cs = const.tile([P, 2, 4 * ROT], BF16, name="cs")
        nc.scalar.dma_start(out=cs[:, 0, :], in_=cos.rearrange("(p i) d -> p (i d)", i=4))
        nc.scalar.dma_start(out=cs[:, 1, :], in_=sin.rearrange("(p i) d -> p (i d)", i=4))
        factors = const.tile([P, 4, 2, ROT], F32, name="ct")

        def load_x(n):
            dst = raw.tile([P, HIDDEN], BF16, name="raw_x%d" % n)
            nc.sync.dma_start(out=dst[:], in_=x[n // 4].rearrange("(p i) k -> p i k", i=4)[:, n % 4, :])
            tiles["raw_x%d" % n] = dst

        def load_down(g):
            dst = raw.tile([P, PACK, CHUNK], BF16, name="raw_wd%d" % g)
            nc.sync.dma_start(
                out=dst[:].rearrange("q (u e) c -> q u (e c)", u=2),
                in_=Wq_d[512 * g : 512 * (g + 1), :].rearrange("(u q e) c -> q u (e c)", u=2, e=2),
            )
            tiles["raw_wd%d" % g] = dst[:]

        def load_up(kind, weight):
            dst = raw.tile([P, PACK, 2 * CHUNK], BF16, name="raw_" + kind)
            nc.sync.dma_start(out=dst[:], in_=weight.rearrange("(j p) c -> p j c", p=P))
            for hg in range(2):
                tiles["raw_%s%d" % (kind, hg)] = dst[:, :, CHUNK * hg : CHUNK * (hg + 1)]

        def tables():
            cos_v = cs[:, 0, :].rearrange("p (i d) -> p i d", d=ROT)
            sin_v = cs[:, 1, :].rearrange("p (i d) -> p i d", d=ROT)
            nc.vector.tensor_copy(out=factors[:, :, 0, :], in_=cos_v)
            nc.vector.tensor_copy(out=factors[:, :, 1, 0:HALF], in_=sin_v[:, :, HALF:ROT])
            nc.vector.tensor_scalar_mul(out=factors[:, :, 1, HALF:ROT], in0=sin_v[:, :, 0:HALF], scalar1=-1.0)

        def regroup(name):
            src = tiles["raw_" + name]
            dst = grp.tile([P, PACK * CHUNK], BF16, tag="gw", name="g_" + name, align_bytes=64)
            tiles["g_" + name] = dst
            view = dst[:].rearrange("p (c j) -> p c j", j=PACK)
            cut = CHUNK - SCALAR_COLS[name[0:2]]
            nc.vector.tensor_copy(
                out=view[:, 0:cut, :].rearrange("p (c r) j -> p c j r", r=4),
                in_=src[:, :, 0:cut].rearrange("p j (c r) -> p c j r", r=4),
            )
            nc.scalar.copy(
                out=view[:, cut:CHUNK, :].rearrange("p (c r) j -> p c j r", r=4),
                in_=src[:, :, cut:CHUNK].rearrange("p j (c r) -> p c j r", r=4),
            )

        def quantise(name, words):
            codes = mx.tile([P, words], U32, name="c_" + name, align_bytes=64)
            scales = mx.tile([P, words], U8, name="s_" + name, align_bytes=64)
            nc.vector.quantize_mx(out=codes[:].bitcast(FP8X4), scales=scales[:], in_=tiles["g_" + name][:])
            tiles["c_" + name] = codes
            tiles["s_" + name] = scales

        def transpose_x(n):
            words = tiles["raw_x%d" % n][:].bitcast(F32)
            for bank in range(2):
                xt = ps_x.tile([P, 4, P], F32, tag="xt", name="xt%d_%d" % (n, bank))
                tiles["xt%d_%d" % (n, bank)] = xt
                for quarter in range(4):
                    first = P * (4 * bank + quarter)
                    nc.tensor.transpose(xt[:, quarter, :], words[:, first : first + P], ident[:])

        def copy_x(n):
            gx = grp.tile([P, PASSES * P * PACK], BF16, tag="gx", name="g_x%d" % n, align_bytes=64)
            tiles["g_x%d" % n] = gx
            view = gx[:].bitcast(F32).rearrange("q (g m u) -> q g m u", g=PASSES, u=2)
            for bank in range(2):
                nc.scalar.copy(
                    out=view[:, 2 * bank : 2 * bank + 2],
                    in_=tiles["xt%d_%d" % (n, bank)][:].rearrange("q (g u) m -> q g m u", u=2),
                )

        def stage1(n):
            qp = ps_q.tile([P, PACK, P], F32, tag="qp", name="qp%d" % n)
            tiles["qp%d" % n] = qp
            for j in range(PACK):
                for g in range(PASSES):
                    nc.tensor.matmul_mx(
                        out=qp[:, j, :],
                        lhsT=tiles["c_wd%d" % g][:, P * j : P * (j + 1)].bitcast(FP8X4),
                        lhsT_scale=tiles["s_wd%d" % g][:, P * j : P * (j + 1)],
                        rhs=tiles["c_x%d" % n][:, P * g : P * (g + 1)].bitcast(FP8X4),
                        rhs_scale=tiles["s_x%d" % n][:, P * g : P * (g + 1)],
                        start=(g == 0),
                        stop=(g == PASSES - 1),
                    )

        def copy_q(n):
            gq = grp.tile([P, P * PACK], BF16, tag="gq", name="g_q%d" % n, align_bytes=64)
            tiles["g_q%d" % n] = gq
            nc.scalar.copy(
                out=gq[:].rearrange("p (m j) -> p m j", j=PACK),
                in_=tiles["qp%d" % n][:].rearrange("p j m -> p m j"),
            )

        def stage2(kind, n, hg):
            acc = psum_of[kind].tile([P, CHUNK], F32, tag=kind, name="%s%d_%d" % (kind, n, hg))
            tiles["%s%d_%d" % (kind, n, hg)] = acc
            nc.tensor.matmul_mx(
                out=acc[:],
                lhsT=tiles["c_q%d" % n][:].bitcast(FP8X4),
                lhsT_scale=tiles["s_q%d" % n][:],
                rhs=tiles["c_%s%d" % (kind, hg)][:].bitcast(FP8X4),
                rhs_scale=tiles["s_%s%d" % (kind, hg)][:],
                start=True,
                stop=True,
            )

        def pair_tile(key, pool, shape, tag):
            if key not in tiles:
                tiles[key] = pool.tile(shape, F32, tag=tag, name=key, align_bytes=64)
            return tiles[key]

        def products(n, hg):
            both = pair_tile("ab%d_%d" % (n // 2, hg), prod, [P, 2, 2, CHUNK], "ab")
            shape = [P, 2, GROUP, ROT]
            nc.vector.tensor_tensor(
                out=both[:, n % 2].rearrange("p f (h d) -> p f h d", d=ROT),
                in0=tiles["rq%d_%d" % (n, hg)][:].rearrange("p (h d) -> p h d", d=ROT).unsqueeze(1).to_broadcast(shape),
                in1=factors[:, n % 4].unsqueeze(2).to_broadcast(shape),
                op=MULT,
            )

        def copy_nope(n, hg):
            done = pair_tile("ot%d_%d" % (n // 2, hg), res, [P, GROUP, 2, 2 * ROT], "ot")
            nc.scalar.copy(
                out=done[:, :, n % 2, ROT : 2 * ROT],
                in_=tiles["np%d_%d" % (n, hg)][:].rearrange("p (h d) -> p h d", d=ROT),
            )

        def add(eng, pair, hg):
            done = pair_tile("ot%d_%d" % (pair, hg), res, [P, GROUP, 2, 2 * ROT], "ot")
            both = tiles["ab%d_%d" % (pair, hg)]
            for half in range(2):
                own = HALF * half
                other = HALF - own
                eng.tensor_tensor(
                    out=done[:, :, :, own : own + HALF].rearrange("p h b d -> p b h d"),
                    in0=both[:, :, 0].rearrange("p b (h d) -> p b h d", d=ROT)[:, :, :, own : own + HALF],
                    in1=both[:, :, 1].rearrange("p b (h d) -> p b h d", d=ROT)[:, :, :, other : other + HALF],
                    op=ADD,
                )

        def store(pair, hg):
            run = 2 * 2 * ROT
            nc.sync.dma_start(
                out=out[pair // 2, GROUP * hg : GROUP * hg + GROUP].rearrange("h (p i) d -> p h (i d)", i=4)[
                    :, :, run * (pair % 2) : run * (pair % 2 + 1)
                ],
                in_=tiles["ot%d_%d" % (pair, hg)][:].rearrange("p h b d -> p h (b d)"),
            )

        load_x(0)
        for g in range(PASSES):
            load_down(g)
        load_x(1)
        load_up("rq", Wrq)
        load_up("np", Wq_nope)
        for n in range(2, BLOCKS):
            load_x(n)

        tables()
        transpose_x(0)
        copy_x(0)
        regroup("wd0")
        quantise("x0", CHUNK)
        for g in range(1, PASSES):
            regroup("wd%d" % g)
            quantise("wd%d" % (g - 1), CHUNK)
        transpose_x(1)
        copy_x(1)
        quantise("wd3", CHUNK)
        stage1(0)
        quantise("x1", CHUNK)
        regroup("rq0")
        quantise("rq0", CHUNK)
        regroup("rq1")
        copy_q(0)
        stage1(1)
        quantise("q0", P)
        quantise("rq1", CHUNK)
        stage2("rq", 0, 0)
        stage2("rq", 0, 1)
        transpose_x(2)

        for n in range(BLOCKS):
            if 1 <= n < BLOCKS - 2:
                stage1(n + 2)
            products(n, 0)
            if n == 0:
                copy_q(1)
                copy_x(2)
                transpose_x(3)
                regroup("np0")
            else:
                copy_nope(n - 1, 0)
                if n + 3 < BLOCKS:
                    copy_x(n + 3)
            if n + 1 < BLOCKS:
                quantise("q%d" % (n + 1), P)
                stage2("rq", n + 1, 0)
                stage2("rq", n + 1, 1)
            if n == 0:
                quantise("x2", CHUNK)
                stage1(2)
            products(n, 1)
            if n == 0:
                quantise("np0", CHUNK)
                regroup("np1")
                copy_x(3)
            else:
                copy_nope(n - 1, 1)
            if n + 2 < BLOCKS:
                copy_q(n + 2)
            if n + 3 < BLOCKS:
                quantise("x%d" % (n + 3), CHUNK)
            if n == 0:
                quantise("np1", CHUNK)
            if n + 4 < BLOCKS:
                transpose_x(n + 4)
            stage2("np", n, 0)
            stage2("np", n, 1)
            if n % 2 == 1:
                add(nc.gpsimd, n // 2, 0)
                add(nc.vector if n == BLOCKS - 1 else nc.gpsimd, n // 2, 1)
            if n >= 2 and n % 2 == 0:
                store(n // 2 - 1, 0)
                store(n // 2 - 1, 1)
        for hg in range(2):
            copy_nope(BLOCKS - 1, hg)
        for hg in range(2):
            store(BLOCKS // 2 - 1, hg)
